import numpy as np
import ml_dtypes


def mxq(x, axis, fmt="e4m3"):
    dtype, down = {"e4m3": (ml_dtypes.float8_e4m3fn, 7), "e5m2": (ml_dtypes.float8_e5m2, 14)}[fmt]
    v = np.moveaxis(np.asarray(x, np.float32).astype(ml_dtypes.bfloat16).astype(np.float64), axis, -1)
    blocks = v.reshape(v.shape[:-1] + (-1, 32))
    amax = np.abs(blocks).max(-1, keepdims=True)
    byte = np.maximum(np.where(amax > 0, np.frexp(amax)[1] - 1 + 127, 0) - down, 1)
    scale = np.exp2(byte - 127.0)
    codes = (blocks / scale).astype(np.float32).astype(dtype).astype(np.float64)
    return np.moveaxis((codes * scale).reshape(v.shape), -1, axis)


WIDE = False


def mx_kscale(k):
    if not WIDE:
        return np.ones(k)
    levels = np.array([10, -10, 5, -5, 0])
    a = np.random.permutation(np.resize(levels, k // 512 * 4)).reshape(k // 512, 4)
    idx = np.arange(k)
    return np.exp2(a[idx // 512, idx % 128 // 32])


BF16 = ml_dtypes.bfloat16


def bf(x):
    return np.asarray(x, np.float32).astype(BF16)


def f64(x):
    return np.asarray(x).astype(np.float64)


B, DIM, D_IN, HID = 2048, 256, 128, 512
D_OUT = DIM - D_IN
LOG_SCALE_CLAMP = 2.0


def _net_draw(c_out):
    k, f = mx_kscale(HID), mx_kscale(HID)
    h = bf(np.maximum(np.random.standard_normal((B, HID)), 0.0) * np.sqrt(2.0) * k)
    w_hid = bf(np.random.standard_normal((HID, HID)) * np.sqrt(2.0 / HID) * f[:, None] / k[None, :])
    b_hid = bf(np.random.standard_normal(HID) * 0.3 * f)
    w_out = bf(np.random.standard_normal((D_OUT, HID)) * c_out / np.sqrt(HID) / f[None, :])
    b_out = bf(np.random.standard_normal(D_OUT) * 0.3)
    return h, w_hid, b_hid, w_out, b_out


def setup_inputs():
    z = bf(np.random.standard_normal((B, DIM)))
    h_s, s_Whid1, s_bhid1, s_Wout, s_bout = _net_draw(1.2)
    h_t, t_Whid1, t_bhid1, t_Wout, t_bout = _net_draw(1.0)
    return {"z": z, "h_s": h_s, "h_t": h_t,
            "s_Whid1": s_Whid1, "s_bhid1": s_bhid1, "s_Wout": s_Wout, "s_bout": s_bout,
            "t_Whid1": t_Whid1, "t_bhid1": t_bhid1, "t_Wout": t_Wout, "t_bout": t_bout}


def _tail(h, w_hid, b_hid, w_out, b_out):
    g = np.maximum((mxq(f64(h), 1, "e4m3") @ mxq(f64(w_hid), 1, "e4m3").T) + f64(b_hid), 0.0)
    return (mxq(g, 1, "e4m3") @ mxq(f64(w_out), 1, "e4m3").T) + f64(b_out)


def reference(z, h_s, h_t, s_Whid1, s_bhid1, s_Wout, s_bout, t_Whid1, t_bhid1, t_Wout, t_bout):
    z = f64(z)
    z1 = z[:, :D_IN]
    z2 = z[:, D_IN:]
    log_s = np.clip(_tail(h_s, s_Whid1, s_bhid1, s_Wout, s_bout), -LOG_SCALE_CLAMP, LOG_SCALE_CLAMP)
    t = _tail(h_t, t_Whid1, t_bhid1, t_Wout, t_bout)
    z2_out = z2 * np.exp(log_s) + t
    z_out = np.concatenate([z1, z2_out], axis=1)
    log_det = log_s.sum(axis=-1)
    return (z_out, log_det)

@@ -1,0 +1,291 @@
+from contextlib import ExitStack
+
+import concourse.mybir as mybir
+from concourse.masks import make_identity
+
+BF16 = mybir.dt.bfloat16
+F32 = mybir.dt.float32
+U32 = mybir.dt.uint32
+U8 = mybir.dt.uint8
+FP8X4 = mybir.dt.float8_e4m3fn_x4
+ALU = mybir.AluOpType
+FN = mybir.ActivationFunctionType
+AXIS = mybir.AxisListType
+
+P = 128
+B = 2048
+DIM = 256
+HID = 512
+D_OUT = 128
+TILES = B // P
+GROUP = 4
+N_GROUPS = TILES // GROUP
+FLOPS = 2 * 2 * B * HID * (HID + D_OUT)
+
+
+def tile_affinecouplinglayer_pa_kernel(
+    tc, z, h_s, h_t, s_Whid1, s_bhid1, s_Wout, s_bout, t_Whid1, t_bhid1, t_Wout, t_bout, out_0, out_1
+):
+    nc = tc.nc
+    h_in = (h_s, h_t)
+    w1_in = (s_Whid1, t_Whid1)
+    b1_in = (s_bhid1, t_bhid1)
+    wo_in = (s_Wout, t_Wout)
+    bo_in = (s_bout, t_bout)
+
+    with ExitStack() as ctx:
+        keep = ctx.enter_context(tc.tile_pool(name="keep", bufs=1))
+        work = ctx.enter_context(tc.tile_pool(name="work", bufs=2))
+        tp = ctx.enter_context(tc.psum_pool(name="tp", bufs=2))
+        l1 = ctx.enter_context(tc.psum_pool(name="l1", bufs=4))
+        l2 = ctx.enter_context(tc.psum_pool(name="l2", bufs=1))
+
+        ident = keep.tile([P, P], F32, name="ident")
+        make_identity(nc, ident[:])
+        warm_in = keep.tile([P, 1], F32, name="warm_in")
+        warm_out = keep.tile([P, 1], F32, name="warm_out")
+        nc.vector.memset(warm_in[:], 0.0)
+        nc.scalar.activation(out=warm_out[:], in_=warm_in[:], func=FN.Exp)
+        ones = keep.tile([P, P], BF16, name="ones")
+        nc.vector.memset(ones[:], 1.0)
+        brow = keep.tile([P, 2 * D_OUT], BF16, name="brow")
+        nc.vector.memset(brow[:], 0.0)
+
+        h_view = [h_in[n].rearrange("(p i) k -> p i k", i=TILES) for n in range(2)]
+        z_view = z.rearrange("(p i) d -> p i d", i=TILES)
+        zo_view = out_0.rearrange("(p i) d -> p i d", i=TILES)
+
+        w1raw = [keep.tile([P, 4 * HID], BF16, name="w1raw%d" % n) for n in range(2)]
+        b1raw = [keep.tile([P, 4], BF16, name="b1raw%d" % n) for n in range(2)]
+        woraw = [keep.tile([P, HID], BF16, name="woraw%d" % n) for n in range(2)]
+        hraw = [[keep.tile([P, GROUP * HID], BF16, name="hraw%d_%d" % (n, g)) for g in range(N_GROUPS)] for n in range(2)]
+        zraw = [keep.tile([P, GROUP * DIM], BF16, name="zraw%d" % g) for g in range(N_GROUPS)]
+
+        def load_w1(n):
+            nc.sync.dma_start(
+                out=w1raw[n][:].rearrange("m (t k) -> m t k", t=4),
+                in_=w1_in[n].rearrange("(m t) k -> m t k", t=4),
+            )
+
+        def load_h(n, g):
+            nc.sync.dma_start(
+                out=hraw[n][g][:].rearrange("p (j k) -> p j k", j=GROUP),
+                in_=h_view[n][:, g * GROUP : (g + 1) * GROUP, :],
+            )
+
+        def load_z(g):
+            nc.sync.dma_start(
+                out=zraw[g][:].rearrange("p (j d) -> p j d", j=GROUP),
+                in_=z_view[:, g * GROUP : (g + 1) * GROUP, :],
+            )
+
+        load_w1(0)
+        load_h(0, 0)
+        nc.sync.dma_start(out=b1raw[0][:], in_=b1_in[0].rearrange("(m t) -> m t", t=4))
+        load_w1(1)
+        load_h(1, 0)
+        nc.sync.dma_start(out=b1raw[1][:], in_=b1_in[1].rearrange("(m t) -> m t", t=4))
+        for n in range(2):
+            nc.sync.dma_start(out=woraw[n][:], in_=wo_in[n])
+        for n in range(2):
+            nc.sync.dma_start(
+                out=brow[0:1, n * D_OUT : (n + 1) * D_OUT], in_=bo_in[n].rearrange("(o c) -> o c", o=1)
+            )
+        for g in range(1, N_GROUPS):
+            load_h(0, g)
+            load_h(1, g)
+            load_z(g - 1)
+        load_z(N_GROUPS - 1)
+
+        def copy_out(engine, out, in_):
+            if engine == "act":
+                nc.scalar.copy(out=out, in_=in_)
+            else:
+                nc.vector.tensor_copy(out=out, in_=in_)
+
+        def transpose_rows(raw, grouped, engines):
+            raw_w = raw[:].bitcast(F32)
+            grouped_w = grouped[:].bitcast(F32)
+            for half in range(2):
+                bank = tp.tile([P, 512], F32, name="bank", tag="tp")
+                for jj in range(2):
+                    j = 2 * half + jj
+                    for u in range(2):
+                        nc.tensor.transpose(
+                            bank[:, u * 256 + jj * P : u * 256 + (jj + 1) * P],
+                            raw_w[:, j * 256 + u * P : j * 256 + (u + 1) * P],
+                            ident[:],
+                        )
+                copy_out(
+                    engines[half],
+                    grouped_w[:, half * 512 : (half + 1) * 512].rearrange("p (c u) -> p c u", u=2),
+                    bank[:].rearrange("p (u c) -> p c u", u=2),
+                )
+
+        def quantise(grouped, codes, scales):
+            nc.vector.quantize_mx(out=codes[:].bitcast(FP8X4), scales=scales[:], in_=grouped[:])
+
+        w1q = [keep.tile([P, HID], U32, name="w1q%d" % n, align_bytes=64) for n in range(2)]
+        w1sc = [keep.tile([P, HID], U8, name="w1sc%d" % n, align_bytes=64) for n in range(2)]
+        b1f = [keep.tile([P, 4], F32, name="b1f%d" % n) for n in range(2)]
+
+        def prep_w1(n):
+            w1g = keep.tile([P, 4 * HID], BF16, name="w1g%d" % n, align_bytes=64)
+            transpose_rows(w1raw[n], w1g, ("act", "dve"))
+            quantise(w1g, w1q[n], w1sc[n])
+            nc.vector.tensor_copy(out=b1f[n][:], in_=b1raw[n][:])
+
+        woq = keep.tile([P, 2 * D_OUT], U32, name="woq", align_bytes=64)
+        wosc = keep.tile([P, 2 * D_OUT], U8, name="wosc", align_bytes=64)
+        bias_bc = keep.tile([P, 2 * D_OUT], F32, name="bias_bc")
+
+        def prep_wout():
+            wog = keep.tile([P, 8 * D_OUT], BF16, name="wog", align_bytes=64)
+            bank = tp.tile([P, 512], F32, name="bank", tag="tp")
+            for n in range(2):
+                words = woraw[n][:].bitcast(F32).rearrange("o (p u) -> o p u", u=2)
+                for u in range(2):
+                    nc.tensor.transpose(
+                        bank[:, u * 256 + n * P : u * 256 + (n + 1) * P], words[:, :, u], ident[:]
+                    )
+            nc.vector.tensor_copy(
+                out=wog[:].bitcast(F32).rearrange("p (c u) -> p c u", u=2),
+                in_=bank[:].rearrange("p (u c) -> p c u", u=2),
+            )
+            quantise(wog, woq, wosc)
+
+        def prep_bias():
+            bank = tp.tile([P, 512], F32, name="bank", tag="tp")
+            nc.tensor.matmul(out=bank[:, 0 : 2 * D_OUT], lhsT=ones[:], rhs=brow[:], start=True, stop=True)
+            nc.vector.tensor_copy(out=bias_bc[:], in_=bank[:, 0 : 2 * D_OUT])
+
+        hq = {}
+        gq = {}
+        ob = {}
+
+        def stage_t(n, g):
+            hg = work.tile([P, GROUP * HID], BF16, name="hg", tag="hg", align_bytes=64)
+            transpose_rows(hraw[n][g], hg, ("act", "act"))
+            codes = work.tile([P, 512], U32, name="hq", tag="hq", bufs=3, align_bytes=64)
+            scales = work.tile([P, 512], U8, name="hsc", tag="hsc", bufs=3, align_bytes=64)
+            quantise(hg, codes, scales)
+            hq[(n, g)] = (codes, scales)
+
+        def stage_l1(n, g):
+            codes, scales = hq[(n, g)]
+            gc = work.tile([P, 4 * 512], BF16, name="gc", tag="gc")
+            for t in range(4):
+                acc = l1.tile([P, 512], F32, name="acc", tag="l1")
+                nc.tensor.matmul_mx(
+                    out=acc[:],
+                    lhsT=w1q[n][:, t * P : (t + 1) * P].bitcast(FP8X4),
+                    lhsT_scale=w1sc[n][:, t * P : (t + 1) * P],
+                    rhs=codes[:].bitcast(FP8X4),
+                    rhs_scale=scales[:],
+                    start=True,
+                    stop=True,
+                )
+                nc.scalar.activation(
+                    out=gc[:, t * 512 : (t + 1) * 512], in_=acc[:], func=FN.Relu, bias=b1f[n][:, t : t + 1]
+                )
+            gg = work.tile([P, 512 * 4], BF16, name="gg", tag="gg", align_bytes=64)
+            nc.vector.tensor_copy(
+                out=gg[:].rearrange("p (c i t) -> p c t i", i=4, t=4),
+                in_=gc[:].rearrange("p (t c i) -> p c t i", t=4, i=4),
+            )
+            gcodes = work.tile([P, 512], U32, name="gq", tag="gq", align_bytes=64)
+            gscales = work.tile([P, 512], U8, name="gsc", tag="gsc", align_bytes=64)
+            quantise(gg, gcodes, gscales)
+            gq[(n, g)] = (gcodes, gscales)
+
+        def stage_l2(n, g):
+            gcodes, gscales = gq[(n, g)]
+            o = l2.tile([P, 512], F32, name="o%d" % n, tag="o%d" % n)
+            for j in range(GROUP):
+                nc.tensor.matmul_mx(
+                    out=o[:, j * P : (j + 1) * P],
+                    lhsT=gcodes[:, j * P : (j + 1) * P].bitcast(FP8X4),
+                    lhsT_scale=gscales[:, j * P : (j + 1) * P],
+                    rhs=woq[:, n * P : (n + 1) * P].bitcast(FP8X4),
+                    rhs_scale=wosc[:, n * P : (n + 1) * P],
+                    start=True,
+                    stop=True,
+                )
+            ob[(n, g)] = o
+
+        ld = keep.tile([P, TILES], F32, name="ld")
+        prod = {}
+        zos = {}
+
+        def by_tile(ap):
+            return ap.rearrange("p (j o) -> p j o", j=GROUP)
+
+        def bias_view(n):
+            return bias_bc[:, n * D_OUT : (n + 1) * D_OUT].unsqueeze(1).to_broadcast([P, GROUP, D_OUT])
+
+        def stage_z1(g):
+            zo = work.tile([P, GROUP * DIM], F32, name="zo", tag="zo", bufs=4)
+            zos[g] = zo
+            nc.gpsimd.tensor_scalar(
+                out=zo[:].rearrange("p (j d) -> p j d", j=GROUP)[:, :, 0:D_OUT],
+                in0=zraw[g][:].rearrange("p (j d) -> p j d", j=GROUP)[:, :, 0:D_OUT],
+                scalar1=1.0,
+                scalar2=0.0,
+                op0=ALU.mult,
+                op1=ALU.add,
+            )
+
+        def stage_es(g):
+            a = work.tile([P, 512], F32, name="a", tag="a")
+            nc.vector.tensor_tensor(out=by_tile(a[:]), in0=by_tile(ob[(0, g)][:]), in1=bias_view(0), op=ALU.add)
+            ls = work.tile([P, 512], F32, name="ls", tag="ls")
+            nc.vector.tensor_scalar(out=ls[:], in0=a[:], scalar1=2.0, scalar2=-2.0, op0=ALU.min, op1=ALU.max)
+            e = work.tile([P, 512], F32, name="e", tag="e")
+            nc.scalar.activation(out=e[:], in_=ls[:], func=FN.Exp)
+            nc.vector.tensor_reduce(
+                out=ld[:, g * GROUP : (g + 1) * GROUP], in_=by_tile(ls[:]), axis=AXIS.X, op=ALU.add
+            )
+            m = work.tile([P, 512], F32, name="m", tag="m")
+            nc.vector.tensor_tensor(
+                out=by_tile(m[:]),
+                in0=by_tile(e[:]),
+                in1=zraw[g][:].rearrange("p (j d) -> p j d", j=GROUP)[:, :, D_OUT:DIM],
+                op=ALU.mult,
+            )
+            prod[g] = m
+
+        def stage_et(g):
+            r = work.tile([P, 512], F32, name="r", tag="r")
+            nc.vector.tensor_tensor(out=by_tile(r[:]), in0=by_tile(ob[(1, g)][:]), in1=bias_view(1), op=ALU.add)
+            zo = zos[g]
+            nc.vector.tensor_tensor(
+                out=zo[:].rearrange("p (j d) -> p j d", j=GROUP)[:, :, D_OUT:DIM],
+                in0=by_tile(r[:]),
+                in1=by_tile(prod[g][:]),
+                op=ALU.add,
+            )
+            nc.sync.dma_start(
+                out=zo_view[:, g * GROUP : (g + 1) * GROUP, :],
+                in_=zo[:].rearrange("p (j d) -> p j d", j=GROUP),
+            )
+
+        units = [(n, g) for g in range(N_GROUPS) for n in range(2)]
+        prep_w1(0)
+        stage_t(*units[0])
+        prep_w1(1)
+        stage_t(*units[1])
+        prep_wout()
+        prep_bias()
+        for i in range(len(units)):
+            n, g = units[i]
+            if i + 2 < len(units):
+                stage_t(*units[i + 2])
+            stage_l1(n, g)
+            if n == 0:
+                stage_z1(g)
+            stage_l2(n, g)
+            if n == 0:
+                stage_es(g)
+            else:
+                stage_et(g)
+        nc.sync.dma_start(out=out_1.rearrange("(p i) -> p i", i=TILES), in_=ld[:])

@@ -18,9 +18,13 @@ DIM = 256
 HID = 512
 D_OUT = 128
 TILES = B // P
-GROUP = 4
-N_GROUPS = TILES // GROUP
+SIZES = [4,4,4,4]
 FLOPS = 2 * 2 * B * HID * (HID + D_OUT)
+PINNED = True
+
+LAG = {'hstep':0.01,'TW0':-6.44,'XW0':-2.21,'QW0':-0.88,'TW1':-1.59,'XW1':-0.21,'QW1':0.18,'TWO':0.62,'XWO':1.14,'QWO':1.34,'BMM':0.92,'XB':1.16,'T':-1.68,'X':-1.19,'QH':-0.55,'L1':-0.46,'RG':0.85,'QG':1.32,'L2':1.44,'G':0.61,'A':1.73,'TS':2.23,'EXP':2.8,'RED':2.42,'D':3,'E':2.56,'F':4.37}
+RG_ON_ACT = []
+X_ON_DVE = []
 
 
 def tile_affinecouplinglayer_pa_kernel(
@@ -32,6 +36,8 @@ def tile_affinecouplinglayer_pa_kernel(
     b1_in = (s_bhid1, t_bhid1)
     wo_in = (s_Wout, t_Wout)
     bo_in = (s_bout, t_bout)
+    starts = [sum(SIZES[:q]) for q in range(len(SIZES))]
+    units = [(n, q) for q in range(len(SIZES)) for n in range(2)]
 
     with ExitStack() as ctx:
         keep = ctx.enter_context(tc.tile_pool(name="keep", bufs=1))
@@ -39,6 +45,8 @@ def tile_affinecouplinglayer_pa_kernel(
         tp = ctx.enter_context(tc.psum_pool(name="tp", bufs=2))
         l1 = ctx.enter_context(tc.psum_pool(name="l1", bufs=4))
         l2 = ctx.enter_context(tc.psum_pool(name="l2", bufs=1))
+        if PINNED:
+            ctx.enter_context(tc.manual_schedule())
 
         ident = keep.tile([P, P], F32, name="ident")
         make_identity(nc, ident[:])
@@ -58,8 +66,8 @@ def tile_affinecouplinglayer_pa_kernel(
         w1raw = [keep.tile([P, 4 * HID], BF16, name="w1raw%d" % n) for n in range(2)]
         b1raw = [keep.tile([P, 4], BF16, name="b1raw%d" % n) for n in range(2)]
         woraw = [keep.tile([P, HID], BF16, name="woraw%d" % n) for n in range(2)]
-        hraw = [[keep.tile([P, GROUP * HID], BF16, name="hraw%d_%d" % (n, g)) for g in range(N_GROUPS)] for n in range(2)]
-        zraw = [keep.tile([P, GROUP * DIM], BF16, name="zraw%d" % g) for g in range(N_GROUPS)]
+        hraw = [keep.tile([P, SIZES[q] * HID], BF16, name="hraw%d_%d" % (n, q)) for (n, q) in units]
+        zraw = [keep.tile([P, SIZES[q] * DIM], BF16, name="zraw%d" % q) for q in range(len(SIZES))]
 
         def load_w1(n):
             nc.sync.dma_start(
@@ -67,35 +75,39 @@ def tile_affinecouplinglayer_pa_kernel(
                 in_=w1_in[n].rearrange("(m t) k -> m t k", t=4),
             )
 
-        def load_h(n, g):
+        def load_b1(n):
+            nc.sync.dma_start(out=b1raw[n][:], in_=b1_in[n].rearrange("(m t) -> m t", t=4))
+
+        def load_h(k):
+            n, q = units[k]
             nc.sync.dma_start(
-                out=hraw[n][g][:].rearrange("p (j k) -> p j k", j=GROUP),
-                in_=h_view[n][:, g * GROUP : (g + 1) * GROUP, :],
+                out=hraw[k][:].rearrange("p (j k) -> p j k", j=SIZES[q]),
+                in_=h_view[n][:, starts[q] : starts[q] + SIZES[q], :],
             )
 
-        def load_z(g):
+        def load_z(q):
             nc.sync.dma_start(
-                out=zraw[g][:].rearrange("p (j d) -> p j d", j=GROUP),
-                in_=z_view[:, g * GROUP : (g + 1) * GROUP, :],
+                out=zraw[q][:].rearrange("p (j d) -> p j d", j=SIZES[q]),
+                in_=z_view[:, starts[q] : starts[q] + SIZES[q], :],
             )
 
         load_w1(0)
-        load_h(0, 0)
-        nc.sync.dma_start(out=b1raw[0][:], in_=b1_in[0].rearrange("(m t) -> m t", t=4))
+        load_h(0)
+        load_b1(0)
         load_w1(1)
-        load_h(1, 0)
-        nc.sync.dma_start(out=b1raw[1][:], in_=b1_in[1].rearrange("(m t) -> m t", t=4))
+        load_h(1)
+        load_b1(1)
         for n in range(2):
             nc.sync.dma_start(out=woraw[n][:], in_=wo_in[n])
         for n in range(2):
             nc.sync.dma_start(
                 out=brow[0:1, n * D_OUT : (n + 1) * D_OUT], in_=bo_in[n].rearrange("(o c) -> o c", o=1)
             )
-        for g in range(1, N_GROUPS):
-            load_h(0, g)
-            load_h(1, g)
-            load_z(g - 1)
-        load_z(N_GROUPS - 1)
+        for q in range(1, len(SIZES)):
+            load_h(2 * q)
+            load_h(2 * q + 1)
+            load_z(q - 1)
+        load_z(len(SIZES) - 1)
 
         def copy_out(engine, out, in_):
             if engine == "act":
@@ -103,189 +115,273 @@ def tile_affinecouplinglayer_pa_kernel(
             else:
                 nc.vector.tensor_copy(out=out, in_=in_)
 
-        def transpose_rows(raw, grouped, engines):
+        def transposes(raw, first, count):
             raw_w = raw[:].bitcast(F32)
-            grouped_w = grouped[:].bitcast(F32)
-            for half in range(2):
-                bank = tp.tile([P, 512], F32, name="bank", tag="tp")
-                for jj in range(2):
-                    j = 2 * half + jj
-                    for u in range(2):
-                        nc.tensor.transpose(
-                            bank[:, u * 256 + jj * P : u * 256 + (jj + 1) * P],
-                            raw_w[:, j * 256 + u * P : j * 256 + (u + 1) * P],
-                            ident[:],
-                        )
-                copy_out(
-                    engines[half],
-                    grouped_w[:, half * 512 : (half + 1) * 512].rearrange("p (c u) -> p c u", u=2),
-                    bank[:].rearrange("p (u c) -> p c u", u=2),
-                )
+            bank = tp.tile([P, 512], F32, name="bank", tag="tp")
+            width = count * P
+            for jj in range(count):
+                j = first + jj
+                for u in range(2):
+                    nc.tensor.transpose(
+                        bank[:, u * width + jj * P : u * width + (jj + 1) * P],
+                        raw_w[:, j * 256 + u * P : j * 256 + (u + 1) * P],
+                        ident[:],
+                    )
+            return bank
+
+        def leave(engine, bank, grouped, first, count):
+            width = count * P
+            copy_out(
+                engine,
+                grouped[:].bitcast(F32)[:, first * 256 : (first + count) * 256].rearrange("p (c u) -> p c u", u=2),
+                bank[:, 0 : 2 * width].rearrange("p (u c) -> p c u", u=2),
+            )
 
         def quantise(grouped, codes, scales):
             nc.vector.quantize_mx(out=codes[:].bitcast(FP8X4), scales=scales[:], in_=grouped[:])
 
+        w1g = [keep.tile([P, 4 * HID], BF16, name="w1g%d" % n, align_bytes=64) for n in range(2)]
         w1q = [keep.tile([P, HID], U32, name="w1q%d" % n, align_bytes=64) for n in range(2)]
         w1sc = [keep.tile([P, HID], U8, name="w1sc%d" % n, align_bytes=64) for n in range(2)]
         b1f = [keep.tile([P, 4], F32, name="b1f%d" % n) for n in range(2)]
-
-        def prep_w1(n):
-            w1g = keep.tile([P, 4 * HID], BF16, name="w1g%d" % n, align_bytes=64)
-            transpose_rows(w1raw[n], w1g, ("act", "dve"))
-            quantise(w1g, w1q[n], w1sc[n])
-            nc.vector.tensor_copy(out=b1f[n][:], in_=b1raw[n][:])
-
+        wog = keep.tile([P, 8 * D_OUT], BF16, name="wog", align_bytes=64)
         woq = keep.tile([P, 2 * D_OUT], U32, name="woq", align_bytes=64)
         wosc = keep.tile([P, 2 * D_OUT], U8, name="wosc", align_bytes=64)
         bias_bc = keep.tile([P, 2 * D_OUT], F32, name="bias_bc")
+        ld = keep.tile([P, TILES], F32, name="ld")
+        st = {}
 
-        def prep_wout():
-            wog = keep.tile([P, 8 * D_OUT], BF16, name="wog", align_bytes=64)
+        def TW(n, h):
+            st[("wb", n, h)] = transposes(w1raw[n], 2 * h, 2)
+
+        def XW(n, h):
+            leave(("act", "dve")[h], st[("wb", n, h)], w1g[n], 2 * h, 2)
+
+        def QW(n):
+            quantise(w1g[n], w1q[n], w1sc[n])
+            nc.vector.tensor_copy(out=b1f[n][:], in_=b1raw[n][:])
+
+        def TWO():
             bank = tp.tile([P, 512], F32, name="bank", tag="tp")
             for n in range(2):
                 words = woraw[n][:].bitcast(F32).rearrange("o (p u) -> o p u", u=2)
                 for u in range(2):
-                    nc.tensor.transpose(
-                        bank[:, u * 256 + n * P : u * 256 + (n + 1) * P], words[:, :, u], ident[:]
-                    )
-            nc.vector.tensor_copy(
-                out=wog[:].bitcast(F32).rearrange("p (c u) -> p c u", u=2),
-                in_=bank[:].rearrange("p (u c) -> p c u", u=2),
-            )
+                    nc.tensor.transpose(bank[:, u * 256 + n * P : u * 256 + (n + 1) * P], words[:, :, u], ident[:])
+            st["wob"] = bank
+
+        def XWO():
+            leave("dve", st["wob"], wog, 0, 2)
+
+        def QWO():
             quantise(wog, woq, wosc)
 
-        def prep_bias():
+        def BMM():
             bank = tp.tile([P, 512], F32, name="bank", tag="tp")
             nc.tensor.matmul(out=bank[:, 0 : 2 * D_OUT], lhsT=ones[:], rhs=brow[:], start=True, stop=True)
-            nc.vector.tensor_copy(out=bias_bc[:], in_=bank[:, 0 : 2 * D_OUT])
+            st["bb"] = bank
 
-        hq = {}
-        gq = {}
-        ob = {}
+        def XB():
+            copy_out("dve", bias_bc[:], st["bb"][:, 0 : 2 * D_OUT])
 
-        def stage_t(n, g):
-            hg = work.tile([P, GROUP * HID], BF16, name="hg", tag="hg", align_bytes=64)
-            transpose_rows(hraw[n][g], hg, ("act", "act"))
-            codes = work.tile([P, 512], U32, name="hq", tag="hq", bufs=3, align_bytes=64)
-            scales = work.tile([P, 512], U8, name="hsc", tag="hsc", bufs=3, align_bytes=64)
-            quantise(hg, codes, scales)
-            hq[(n, g)] = (codes, scales)
+        def size(k):
+            return SIZES[units[k][1]]
 
-        def stage_l1(n, g):
-            codes, scales = hq[(n, g)]
-            gc = work.tile([P, 4 * 512], BF16, name="gc", tag="gc")
-            for t in range(4):
-                acc = l1.tile([P, 512], F32, name="acc", tag="l1")
-                nc.tensor.matmul_mx(
-                    out=acc[:],
-                    lhsT=w1q[n][:, t * P : (t + 1) * P].bitcast(FP8X4),
-                    lhsT_scale=w1sc[n][:, t * P : (t + 1) * P],
-                    rhs=codes[:].bitcast(FP8X4),
-                    rhs_scale=scales[:],
-                    start=True,
-                    stop=True,
-                )
-                nc.scalar.activation(
-                    out=gc[:, t * 512 : (t + 1) * 512], in_=acc[:], func=FN.Relu, bias=b1f[n][:, t : t + 1]
-                )
-            gg = work.tile([P, 512 * 4], BF16, name="gg", tag="gg", align_bytes=64)
-            nc.vector.tensor_copy(
-                out=gg[:].rearrange("p (c i t) -> p c t i", i=4, t=4),
-                in_=gc[:].rearrange("p (t c i) -> p c t i", t=4, i=4),
+        def T(k, h):
+            if h == 0:
+                st[("hg", k)] = work.tile([P, size(k) * HID], BF16, name="hg", tag="hg", align_bytes=64)
+            st[("tb", k, h)] = transposes(hraw[k], 2 * h, min(2, size(k) - 2 * h))
+
+        def X(k, h):
+            engine = "dve" if [k, h] in X_ON_DVE else "act"
+            leave(engine, st[("tb", k, h)], st[("hg", k)], 2 * h, min(2, size(k) - 2 * h))
+
+        def QH(k):
+            cols = size(k) * P
+            codes = work.tile([P, cols], U32, name="hq", tag="hq", bufs=3, align_bytes=64)
+            scales = work.tile([P, cols], U8, name="hsc", tag="hsc", bufs=3, align_bytes=64)
+            quantise(st[("hg", k)], codes, scales)
+            st[("hq", k)] = (codes, scales)
+
+        def L1(k, t):
+            n = units[k][0]
+            cols = size(k) * P
+            per = 512 // cols
+            if t % per == 0:
+                st[("acc", k, t // per)] = l1.tile([P, 512], F32, name="acc", tag="l1")
+            acc = st[("acc", k, t // per)]
+            codes, scales = st[("hq", k)]
+            nc.tensor.matmul_mx(
+                out=acc[:, (t % per) * cols : (t % per + 1) * cols],
+                lhsT=w1q[n][:, t * P : (t + 1) * P].bitcast(FP8X4),
+                lhsT_scale=w1sc[n][:, t * P : (t + 1) * P],
+                rhs=codes[:].bitcast(FP8X4),
+                rhs_scale=scales[:],
+                start=True,
+                stop=True,
             )
-            gcodes = work.tile([P, 512], U32, name="gq", tag="gq", align_bytes=64)
-            gscales = work.tile([P, 512], U8, name="gsc", tag="gsc", align_bytes=64)
-            quantise(gg, gcodes, gscales)
-            gq[(n, g)] = (gcodes, gscales)
 
-        def stage_l2(n, g):
-            gcodes, gscales = gq[(n, g)]
+        def R(k, t):
+            n = units[k][0]
+            cols = size(k) * P
+            per = 512 // cols
+            if t == 0:
+                st[("gc", k)] = work.tile([P, 4 * cols], BF16, name="gc", tag="gc")
+            nc.scalar.activation(
+                out=st[("gc", k)][:, t * cols : (t + 1) * cols],
+                in_=st[("acc", k, t // per)][:, (t % per) * cols : (t % per + 1) * cols],
+                func=FN.Relu,
+                bias=b1f[n][:, t : t + 1],
+            )
+
+        def RG(k):
+            cols = size(k) * P
+            gg = work.tile([P, cols * 4], BF16, name="gg", tag="gg", align_bytes=64)
+            copy_out(
+                "act" if k in RG_ON_ACT else "dve",
+                gg[:].rearrange("p (c i t) -> p c t i", i=4, t=4),
+                st[("gc", k)][:].rearrange("p (t c i) -> p c t i", t=4, i=4),
+            )
+            st[("gg", k)] = gg
+
+        def QG(k):
+            cols = size(k) * P
+            codes = work.tile([P, cols], U32, name="gq", tag="gq", align_bytes=64)
+            scales = work.tile([P, cols], U8, name="gsc", tag="gsc", align_bytes=64)
+            quantise(st[("gg", k)], codes, scales)
+            st[("gq", k)] = (codes, scales)
+
+        def L2(k):
+            n = units[k][0]
+            codes, scales = st[("gq", k)]
             o = l2.tile([P, 512], F32, name="o%d" % n, tag="o%d" % n)
-            for j in range(GROUP):
+            for j in range(size(k)):
                 nc.tensor.matmul_mx(
                     out=o[:, j * P : (j + 1) * P],
-                    lhsT=gcodes[:, j * P : (j + 1) * P].bitcast(FP8X4),
-                    lhsT_scale=gscales[:, j * P : (j + 1) * P],
+                    lhsT=codes[:, j * P : (j + 1) * P].bitcast(FP8X4),
+                    lhsT_scale=scales[:, j * P : (j + 1) * P],
                     rhs=woq[:, n * P : (n + 1) * P].bitcast(FP8X4),
                     rhs_scale=wosc[:, n * P : (n + 1) * P],
                     start=True,
                     stop=True,
                 )
-            ob[(n, g)] = o
+            st[("o", k)] = o
 
-        ld = keep.tile([P, TILES], F32, name="ld")
-        prod = {}
-        zos = {}
+        def by_tile(ap, q):
+            return ap.rearrange("p (j o) -> p j o", j=SIZES[q])
 
-        def by_tile(ap):
-            return ap.rearrange("p (j o) -> p j o", j=GROUP)
+        def bias_view(n, q):
+            return bias_bc[:, n * D_OUT : (n + 1) * D_OUT].unsqueeze(1).to_broadcast([P, SIZES[q], D_OUT])
 
-        def bias_view(n):
-            return bias_bc[:, n * D_OUT : (n + 1) * D_OUT].unsqueeze(1).to_broadcast([P, GROUP, D_OUT])
+        def ep_tile(name, q):
+            return work.tile([P, SIZES[q] * D_OUT], F32, name=name, tag=name)
 
-        def stage_z1(g):
-            zo = work.tile([P, GROUP * DIM], F32, name="zo", tag="zo", bufs=4)
-            zos[g] = zo
+        def G(q):
+            zo = work.tile([P, SIZES[q] * DIM], F32, name="zo", tag="zo", bufs=4)
+            st[("zo", q)] = zo
             nc.gpsimd.tensor_scalar(
-                out=zo[:].rearrange("p (j d) -> p j d", j=GROUP)[:, :, 0:D_OUT],
-                in0=zraw[g][:].rearrange("p (j d) -> p j d", j=GROUP)[:, :, 0:D_OUT],
+                out=zo[:].rearrange("p (j d) -> p j d", j=SIZES[q])[:, :, 0:D_OUT],
+                in0=zraw[q][:].rearrange("p (j d) -> p j d", j=SIZES[q])[:, :, 0:D_OUT],
                 scalar1=1.0,
                 scalar2=0.0,
                 op0=ALU.mult,
                 op1=ALU.add,
             )
 
-        def stage_es(g):
-            a = work.tile([P, 512], F32, name="a", tag="a")
-            nc.vector.tensor_tensor(out=by_tile(a[:]), in0=by_tile(ob[(0, g)][:]), in1=bias_view(0), op=ALU.add)
-            ls = work.tile([P, 512], F32, name="ls", tag="ls")
-            nc.vector.tensor_scalar(out=ls[:], in0=a[:], scalar1=2.0, scalar2=-2.0, op0=ALU.min, op1=ALU.max)
-            e = work.tile([P, 512], F32, name="e", tag="e")
-            nc.scalar.activation(out=e[:], in_=ls[:], func=FN.Exp)
-            nc.vector.tensor_reduce(
-                out=ld[:, g * GROUP : (g + 1) * GROUP], in_=by_tile(ls[:]), axis=AXIS.X, op=ALU.add
-            )
-            m = work.tile([P, 512], F32, name="m", tag="m")
+        def A(q):
+            a = ep_tile("a", q)
             nc.vector.tensor_tensor(
-                out=by_tile(m[:]),
-                in0=by_tile(e[:]),
-                in1=zraw[g][:].rearrange("p (j d) -> p j d", j=GROUP)[:, :, D_OUT:DIM],
+                out=by_tile(a[:], q), in0=by_tile(st[("o", 2 * q)][:, 0 : SIZES[q] * D_OUT], q), in1=bias_view(0, q), op=ALU.add
+            )
+            st[("a", q)] = a
+
+        def TS(q):
+            ls = ep_tile("ls", q)
+            nc.vector.tensor_scalar(
+                out=ls[:], in0=st[("a", q)][:], scalar1=2.0, scalar2=-2.0, op0=ALU.min, op1=ALU.max
+            )
+            st[("ls", q)] = ls
+
+        def EXP(q):
+            e = ep_tile("e", q)
+            nc.scalar.activation(out=e[:], in_=st[("ls", q)][:], func=FN.Exp)
+            st[("e", q)] = e
+
+        def RED(q):
+            nc.vector.tensor_reduce(
+                out=ld[:, starts[q] : starts[q] + SIZES[q]], in_=by_tile(st[("ls", q)][:], q), axis=AXIS.X, op=ALU.add
+            )
+
+        def D(q):
+            m = ep_tile("m", q)
+            nc.vector.tensor_tensor(
+                out=by_tile(m[:], q),
+                in0=by_tile(st[("e", q)][:], q),
+                in1=zraw[q][:].rearrange("p (j d) -> p j d", j=SIZES[q])[:, :, D_OUT:DIM],
                 op=ALU.mult,
             )
-            prod[g] = m
+            st[("m", q)] = m
 
-        def stage_et(g):
-            r = work.tile([P, 512], F32, name="r", tag="r")
-            nc.vector.tensor_tensor(out=by_tile(r[:]), in0=by_tile(ob[(1, g)][:]), in1=bias_view(1), op=ALU.add)
-            zo = zos[g]
+        def E(q):
+            r = ep_tile("r", q)
             nc.vector.tensor_tensor(
-                out=zo[:].rearrange("p (j d) -> p j d", j=GROUP)[:, :, D_OUT:DIM],
-                in0=by_tile(r[:]),
-                in1=by_tile(prod[g][:]),
+                out=by_tile(r[:], q), in0=by_tile(st[("o", 2 * q + 1)][:, 0 : SIZES[q] * D_OUT], q), in1=bias_view(1, q), op=ALU.add
+            )
+            st[("r", q)] = r
+
+        def F(q):
+            nc.vector.tensor_tensor(
+                out=st[("zo", q)][:].rearrange("p (j d) -> p j d", j=SIZES[q])[:, :, D_OUT:DIM],
+                in0=by_tile(st[("r", q)][:], q),
+                in1=by_tile(st[("m", q)][:], q),
                 op=ALU.add,
             )
+
+        def ST(q):
             nc.sync.dma_start(
-                out=zo_view[:, g * GROUP : (g + 1) * GROUP, :],
-                in_=zo[:].rearrange("p (j d) -> p j d", j=GROUP),
+                out=zo_view[:, starts[q] : starts[q] + SIZES[q], :],
+                in_=st[("zo", q)][:].rearrange("p (j d) -> p j d", j=SIZES[q]),
             )
 
-        units = [(n, g) for g in range(N_GROUPS) for n in range(2)]
-        prep_w1(0)
-        stage_t(*units[0])
-        prep_w1(1)
-        stage_t(*units[1])
-        prep_wout()
-        prep_bias()
-        for i in range(len(units)):
-            n, g = units[i]
-            if i + 2 < len(units):
-                stage_t(*units[i + 2])
-            stage_l1(n, g)
-            if n == 0:
-                stage_z1(g)
-            stage_l2(n, g)
-            if n == 0:
-                stage_es(g)
-            else:
-                stage_et(g)
+        plan = []
+
+        def at(position, fn, *args):
+            plan.append((position, len(plan), fn, args))
+
+        step = LAG["hstep"]
+        for n in range(2):
+            for h in range(2):
+                at(LAG["TW%d" % n] + h * step, TW, n, h)
+                at(LAG["XW%d" % n] + h * step, XW, n, h)
+            at(LAG["QW%d" % n], QW, n)
+        at(LAG["TWO"], TWO)
+        at(LAG["XWO"], XWO)
+        at(LAG["QWO"], QWO)
+        at(LAG["BMM"], BMM)
+        at(LAG["XB"], XB)
+        for k in range(len(units)):
+            for h in range((size(k) + 1) // 2):
+                at(k + LAG["T"] + h * step, T, k, h)
+                at(k + LAG["X"] + h * step, X, k, h)
+            at(k + LAG["QH"], QH, k)
+            for t in range(4):
+                at(k + LAG["L1"] + t * 0.25, L1, k, t)
+                at(k + t * 0.25, R, k, t)
+            at(k + LAG["RG"], RG, k)
+            at(k + LAG["QG"], QG, k)
+            at(k + LAG["L2"], L2, k)
+        for q in range(len(SIZES)):
+            ks = 2 * q
+            kt = 2 * q + 1
+            at(ks + LAG["G"], G, q)
+            at(ks + LAG["A"], A, q)
+            at(ks + LAG["TS"], TS, q)
+            at(ks + LAG["EXP"], EXP, q)
+            at(ks + LAG["RED"], RED, q)
+            at(ks + LAG["D"], D, q)
+            at(kt + LAG["E"], E, q)
+            last = max(kt + LAG["F"], ks + LAG["D"] + 0.001, ks + LAG["G"] + 0.001)
+            at(last, F, q)
+            at(last + 0.001, ST, q)
+        for entry in sorted(plan, key=lambda e: (e[0], e[1])):
+            entry[2](*entry[3])
         nc.sync.dma_start(out=out_1.rearrange("(p i) -> p i", i=TILES), in_=ld[:])

@@ -18,12 +18,12 @@ DIM = 256
 HID = 512
 D_OUT = 128
 TILES = B // P
-SIZES = [4,4,4,4]
+SIZES = [4,4,4,2,2]
 FLOPS = 2 * 2 * B * HID * (HID + D_OUT)
 PINNED = True
 
-LAG = {'hstep':0.01,'TW0':-6.44,'XW0':-2.21,'QW0':-0.88,'TW1':-1.59,'XW1':-0.21,'QW1':0.18,'TWO':0.62,'XWO':1.14,'QWO':1.34,'BMM':0.92,'XB':1.16,'T':-1.68,'X':-1.19,'QH':-0.55,'L1':-0.46,'RG':0.85,'QG':1.32,'L2':1.44,'G':0.61,'A':1.73,'TS':2.23,'EXP':2.8,'RED':2.42,'D':3,'E':2.56,'F':4.37}
-RG_ON_ACT = []
+LAG = {'hstep':0.01,'TW0':-5.511,'XW0':-4.472,'QW0':-2.322,'TW1':-1.055,'XW1':-0.548,'QW1':-0.076,'TWO':0.368,'XWO':0.512,'QWO':1.542,'BMM':0.599,'XB':1.42,'T':-1.339,'X':-1.163,'QH':-0.579,'L1':-0.272,'RG':0.142,'QG':0.669,'L2':1.023,'G':2.766,'A':1.08,'TS':1.417,'EXP':1.606,'RED':3.009,'D':1.956,'E':1.375,'F':-0.733}
+RG_ON_ACT = [8,9]
 X_ON_DVE = []
 
 
@@ -276,7 +276,7 @@ def tile_affinecouplinglayer_pa_kernel(
             return work.tile([P, SIZES[q] * D_OUT], F32, name=name, tag=name)
 
         def G(q):
-            zo = work.tile([P, SIZES[q] * DIM], F32, name="zo", tag="zo", bufs=4)
+            zo = work.tile([P, SIZES[q] * DIM], F32, name="zo", tag="zo", bufs=5)
             st[("zo", q)] = zo
             nc.gpsimd.tensor_scalar(
                 out=zo[:].rearrange("p (j d) -> p j d", j=SIZES[q])[:, :, 0:D_OUT],
@@ -348,6 +348,8 @@ def tile_affinecouplinglayer_pa_kernel(
             plan.append((position, len(plan), fn, args))
 
         step = LAG["hstep"]
+        width = [size(k) / 4.0 for k in range(len(units))]
+        begin = [sum(width[:k]) for k in range(len(units))]
         for n in range(2):
             for h in range(2):
                 at(LAG["TW%d" % n] + h * step, TW, n, h)
@@ -360,18 +362,19 @@ def tile_affinecouplinglayer_pa_kernel(
         at(LAG["XB"], XB)
         for k in range(len(units)):
             for h in range((size(k) + 1) // 2):
-                at(k + LAG["T"] + h * step, T, k, h)
-                at(k + LAG["X"] + h * step, X, k, h)
-            at(k + LAG["QH"], QH, k)
+                at(begin[k] + LAG["T"] + h * step, T, k, h)
+                at(begin[k] + LAG["X"] + h * step, X, k, h)
+            at(begin[k] + LAG["QH"], QH, k)
             for t in range(4):
-                at(k + LAG["L1"] + t * 0.25, L1, k, t)
-                at(k + t * 0.25, R, k, t)
-            at(k + LAG["RG"], RG, k)
-            at(k + LAG["QG"], QG, k)
-            at(k + LAG["L2"], L2, k)
+                at(begin[k] + LAG["L1"] + t * 0.25 * width[k], L1, k, t)
+                at(begin[k] + t * 0.25 * width[k], R, k, t)
+            end = begin[k] + width[k]
+            at(end + LAG["RG"], RG, k)
+            at(end + LAG["QG"], QG, k)
+            at(end + LAG["L2"], L2, k)
         for q in range(len(SIZES)):
-            ks = 2 * q
-            kt = 2 * q + 1
+            ks = begin[2 * q] + width[2 * q]
+            kt = begin[2 * q + 1] + width[2 * q + 1]
             at(ks + LAG["G"], G, q)
             at(ks + LAG["A"], A, q)
             at(ks + LAG["TS"], TS, q)
@@ -379,7 +382,7 @@ def tile_affinecouplinglayer_pa_kernel(
             at(ks + LAG["RED"], RED, q)
             at(ks + LAG["D"], D, q)
             at(kt + LAG["E"], E, q)
-            last = max(kt + LAG["F"], ks + LAG["D"] + 0.001, ks + LAG["G"] + 0.001)
+            last = max(kt + LAG["F"], ks + LAG["D"] + 0.001, ks + LAG["G"] + 0.001, kt + LAG["E"] + 0.001)
             at(last, F, q)
             at(last + 0.001, ST, q)
         for entry in sorted(plan, key=lambda e: (e[0], e[1])):

@@ -18,13 +18,13 @@ DIM = 256
 HID = 512
 D_OUT = 128
 TILES = B // P
-SIZES = [4,4,4,2,2]
+SIZES = [4,4,4,4]
 FLOPS = 2 * 2 * B * HID * (HID + D_OUT)
 PINNED = True
 
-LAG = {'hstep':0.01,'TW0':-5.511,'XW0':-4.472,'QW0':-2.322,'TW1':-1.055,'XW1':-0.548,'QW1':-0.076,'TWO':0.368,'XWO':0.512,'QWO':1.542,'BMM':0.599,'XB':1.42,'T':-1.339,'X':-1.163,'QH':-0.579,'L1':-0.272,'RG':0.142,'QG':0.669,'L2':1.023,'G':2.766,'A':1.08,'TS':1.417,'EXP':1.606,'RED':3.009,'D':1.956,'E':1.375,'F':-0.733}
-RG_ON_ACT = [8,9]
-X_ON_DVE = []
+LAG = {'hstep':0.01,'TW0':-6.44,'XW0':-2.21,'QW0':-0.88,'TW1':-1.59,'XW1':-0.21,'QW1':0.18,'TWO':0.62,'XWO':1.14,'QWO':1.34,'BMM':0.92,'XB':1.16,'T':-1.68,'X':-1.19,'QH':-0.55,'L1':-0.46,'RG':0.85,'QG':1.32,'L2':1.44,'G':0.61,'A':1.73,'TS':2.23,'EXP':2.8,'RED':2.42,'D':3,'E':2.56,'F':4.37}
+RG_ON_ACT = []
+X_ON_DVE = [[1, 1], [3, 1], [5, 1], [7, 1]]
 
 
 def tile_affinecouplinglayer_pa_kernel(
@@ -276,7 +276,7 @@ def tile_affinecouplinglayer_pa_kernel(
             return work.tile([P, SIZES[q] * D_OUT], F32, name=name, tag=name)
 
         def G(q):
-            zo = work.tile([P, SIZES[q] * DIM], F32, name="zo", tag="zo", bufs=5)
+            zo = work.tile([P, SIZES[q] * DIM], F32, name="zo", tag="zo", bufs=4)
             st[("zo", q)] = zo
             nc.gpsimd.tensor_scalar(
                 out=zo[:].rearrange("p (j d) -> p j d", j=SIZES[q])[:, :, 0:D_OUT],
@@ -348,8 +348,6 @@ def tile_affinecouplinglayer_pa_kernel(
             plan.append((position, len(plan), fn, args))
 
         step = LAG["hstep"]
-        width = [size(k) / 4.0 for k in range(len(units))]
-        begin = [sum(width[:k]) for k in range(len(units))]
         for n in range(2):
             for h in range(2):
                 at(LAG["TW%d" % n] + h * step, TW, n, h)
@@ -362,19 +360,18 @@ def tile_affinecouplinglayer_pa_kernel(
         at(LAG["XB"], XB)
         for k in range(len(units)):
             for h in range((size(k) + 1) // 2):
-                at(begin[k] + LAG["T"] + h * step, T, k, h)
-                at(begin[k] + LAG["X"] + h * step, X, k, h)
-            at(begin[k] + LAG["QH"], QH, k)
+                at(k + LAG["T"] + h * step, T, k, h)
+                at(k + LAG["X"] + h * step, X, k, h)
+            at(k + LAG["QH"], QH, k)
             for t in range(4):
-                at(begin[k] + LAG["L1"] + t * 0.25 * width[k], L1, k, t)
-                at(begin[k] + t * 0.25 * width[k], R, k, t)
-            end = begin[k] + width[k]
-            at(end + LAG["RG"], RG, k)
-            at(end + LAG["QG"], QG, k)
-            at(end + LAG["L2"], L2, k)
+                at(k + LAG["L1"] + t * 0.25, L1, k, t)
+                at(k + t * 0.25, R, k, t)
+            at(k + LAG["RG"], RG, k)
+            at(k + LAG["QG"], QG, k)
+            at(k + LAG["L2"], L2, k)
         for q in range(len(SIZES)):
-            ks = begin[2 * q] + width[2 * q]
-            kt = begin[2 * q + 1] + width[2 * q + 1]
+            ks = 2 * q
+            kt = 2 * q + 1
             at(ks + LAG["G"], G, q)
             at(ks + LAG["A"], A, q)
             at(ks + LAG["TS"], TS, q)
@@ -382,7 +379,7 @@ def tile_affinecouplinglayer_pa_kernel(
             at(ks + LAG["RED"], RED, q)
             at(ks + LAG["D"], D, q)
             at(kt + LAG["E"], E, q)
-            last = max(kt + LAG["F"], ks + LAG["D"] + 0.001, ks + LAG["G"] + 0.001, kt + LAG["E"] + 0.001)
+            last = max(kt + LAG["F"], ks + LAG["D"] + 0.001, ks + LAG["G"] + 0.001)
             at(last, F, q)
             at(last + 0.001, ST, q)
         for entry in sorted(plan, key=lambda e: (e[0], e[1])):

@@ -22,9 +22,9 @@ SIZES = [4,4,4,4]
 FLOPS = 2 * 2 * B * HID * (HID + D_OUT)
 PINNED = True
 
-LAG = {'hstep':0.01,'TW0':-6.44,'XW0':-2.21,'QW0':-0.88,'TW1':-1.59,'XW1':-0.21,'QW1':0.18,'TWO':0.62,'XWO':1.14,'QWO':1.34,'BMM':0.92,'XB':1.16,'T':-1.68,'X':-1.19,'QH':-0.55,'L1':-0.46,'RG':0.85,'QG':1.32,'L2':1.44,'G':0.61,'A':1.73,'TS':2.23,'EXP':2.8,'RED':2.42,'D':3,'E':2.56,'F':4.37}
+LAG = {'hstep':0.01,'TW0':-6.44,'XW0':-2.21,'QW0':-0.88,'TW1':-1.59,'XW1':-0.21,'QW1':0.18,'TWO':0.62,'XWO':1.14,'QWO':1.34,'BMM':0.92,'XB':1.16,'T':-1.68,'X':-1.19,'QH':-0.55,'L1':-0.46,'RG':0.85,'QG':1.32,'L2':1.44,'G':0.61,'A':1.73,'TS':2.23,'EXP':2.8,'D':3.55,'E':2.56,'F':4.37,'LD':2.45,'LDX':2.86,'ET':3.31}
 RG_ON_ACT = []
-X_ON_DVE = [[1, 1], [3, 1], [5, 1], [7, 1]]
+X_ON_DVE = []
 
 
 def tile_affinecouplinglayer_pa_kernel(
@@ -42,8 +42,8 @@ def tile_affinecouplinglayer_pa_kernel(
     with ExitStack() as ctx:
         keep = ctx.enter_context(tc.tile_pool(name="keep", bufs=1))
         work = ctx.enter_context(tc.tile_pool(name="work", bufs=2))
-        tp = ctx.enter_context(tc.psum_pool(name="tp", bufs=2))
-        l1 = ctx.enter_context(tc.psum_pool(name="l1", bufs=4))
+        tp = ctx.enter_context(tc.psum_pool(name="tp", bufs=3))
+        l1 = ctx.enter_context(tc.psum_pool(name="l1", bufs=3))
         l2 = ctx.enter_context(tc.psum_pool(name="l2", bufs=1))
         if PINNED:
             ctx.enter_context(tc.manual_schedule())
@@ -56,6 +56,8 @@ def tile_affinecouplinglayer_pa_kernel(
         nc.scalar.activation(out=warm_out[:], in_=warm_in[:], func=FN.Exp)
         ones = keep.tile([P, P], BF16, name="ones")
         nc.vector.memset(ones[:], 1.0)
+        ones_f = keep.tile([P, 2], F32, name="ones_f")
+        nc.vector.memset(ones_f[:], 1.0)
         brow = keep.tile([P, 2 * D_OUT], BF16, name="brow")
         nc.vector.memset(brow[:], 0.0)
 
@@ -66,6 +68,8 @@ def tile_affinecouplinglayer_pa_kernel(
         w1raw = [keep.tile([P, 4 * HID], BF16, name="w1raw%d" % n) for n in range(2)]
         b1raw = [keep.tile([P, 4], BF16, name="b1raw%d" % n) for n in range(2)]
         woraw = [keep.tile([P, HID], BF16, name="woraw%d" % n) for n in range(2)]
+        bsraw = keep.tile([P, 1], BF16, name="bsraw")
+        bscol = keep.tile([P, 1], F32, name="bscol")
         hraw = [keep.tile([P, SIZES[q] * HID], BF16, name="hraw%d_%d" % (n, q)) for (n, q) in units]
         zraw = [keep.tile([P, SIZES[q] * DIM], BF16, name="zraw%d" % q) for q in range(len(SIZES))]
 
@@ -103,6 +107,7 @@ def tile_affinecouplinglayer_pa_kernel(
             nc.sync.dma_start(
                 out=brow[0:1, n * D_OUT : (n + 1) * D_OUT], in_=bo_in[n].rearrange("(o c) -> o c", o=1)
             )
+        nc.sync.dma_start(out=bsraw[:], in_=bo_in[0].rearrange("(o c) -> o c", c=1))
         for q in range(1, len(SIZES)):
             load_h(2 * q)
             load_h(2 * q + 1)
@@ -182,6 +187,7 @@ def tile_affinecouplinglayer_pa_kernel(
 
         def XB():
             copy_out("dve", bias_bc[:], st["bb"][:, 0 : 2 * D_OUT])
+            nc.vector.tensor_copy(out=bscol[:], in_=bsraw[:])
 
         def size(k):
             return SIZES[units[k][1]]
@@ -254,6 +260,18 @@ def tile_affinecouplinglayer_pa_kernel(
             n = units[k][0]
             codes, scales = st[("gq", k)]
             o = l2.tile([P, 512], F32, name="o%d" % n, tag="o%d" % n)
+            st[("o", k)] = o
+            if n == 0:
+                nc.tensor.matmul_mx(
+                    out=o[:, 0 : size(k) * P],
+                    lhsT=woq[:, 0:P].bitcast(FP8X4),
+                    lhsT_scale=wosc[:, 0:P],
+                    rhs=codes[:].bitcast(FP8X4),
+                    rhs_scale=scales[:],
+                    start=True,
+                    stop=True,
+                )
+                return
             for j in range(size(k)):
                 nc.tensor.matmul_mx(
                     out=o[:, j * P : (j + 1) * P],
@@ -289,16 +307,14 @@ def tile_affinecouplinglayer_pa_kernel(
 
         def A(q):
             a = ep_tile("a", q)
-            nc.vector.tensor_tensor(
-                out=by_tile(a[:], q), in0=by_tile(st[("o", 2 * q)][:, 0 : SIZES[q] * D_OUT], q), in1=bias_view(0, q), op=ALU.add
+            nc.vector.tensor_scalar(
+                out=a[:], in0=st[("o", 2 * q)][:, 0 : SIZES[q] * D_OUT], scalar1=bscol[:, 0:1], scalar2=2.0, op0=ALU.add, op1=ALU.min
             )
             st[("a", q)] = a
 
         def TS(q):
             ls = ep_tile("ls", q)
-            nc.vector.tensor_scalar(
-                out=ls[:], in0=st[("a", q)][:], scalar1=2.0, scalar2=-2.0, op0=ALU.min, op1=ALU.max
-            )
+            nc.vector.tensor_scalar_max(out=ls[:], in0=st[("a", q)][:], scalar1=-2.0)
             st[("ls", q)] = ls
 
         def EXP(q):
@@ -306,16 +322,35 @@ def tile_affinecouplinglayer_pa_kernel(
             nc.scalar.activation(out=e[:], in_=st[("ls", q)][:], func=FN.Exp)
             st[("e", q)] = e
 
-        def RED(q):
-            nc.vector.tensor_reduce(
-                out=ld[:, starts[q] : starts[q] + SIZES[q]], in_=by_tile(st[("ls", q)][:], q), axis=AXIS.X, op=ALU.add
+        def LD(q):
+            bank = tp.tile([P, 512], F32, name="bank", tag="tp")
+            for j in range(SIZES[q]):
+                nc.tensor.matmul(
+                    out=bank[:, 2 * j : 2 * j + 2],
+                    lhsT=st[("ls", q)][:, j * P : (j + 1) * P],
+                    rhs=ones_f[:],
+                    start=True,
+                    stop=True,
+                )
+            st[("ldb", q)] = bank
+
+        def LDX(q):
+            nc.vector.tensor_copy(
+                out=ld[:, starts[q] : starts[q] + SIZES[q]],
+                in_=st[("ldb", q)][:, 0 : 2 * SIZES[q]].rearrange("p (j c) -> p j c", c=2)[:, :, 0],
             )
+
+        def ET(q):
+            bank = tp.tile([P, 512], F32, name="bank", tag="tp")
+            for j in range(SIZES[q]):
+                nc.tensor.transpose(bank[:, j * P : (j + 1) * P], st[("e", q)][:, j * P : (j + 1) * P], ident[:])
+            st[("eb", q)] = bank
 
         def D(q):
             m = ep_tile("m", q)
             nc.vector.tensor_tensor(
                 out=by_tile(m[:], q),
-                in0=by_tile(st[("e", q)][:], q),
+                in0=by_tile(st[("eb", q)][:, 0 : SIZES[q] * D_OUT], q),
                 in1=zraw[q][:].rearrange("p (j d) -> p j d", j=SIZES[q])[:, :, D_OUT:DIM],
                 op=ALU.mult,
             )
@@ -376,7 +411,9 @@ def tile_affinecouplinglayer_pa_kernel(
             at(ks + LAG["A"], A, q)
             at(ks + LAG["TS"], TS, q)
             at(ks + LAG["EXP"], EXP, q)
-            at(ks + LAG["RED"], RED, q)
+            at(ks + LAG["LD"], LD, q)
+            at(ks + LAG["LDX"], LDX, q)
+            at(ks + LAG["ET"], ET, q)
             at(ks + LAG["D"], D, q)
             at(kt + LAG["E"], E, q)
             last = max(kt + LAG["F"], ks + LAG["D"] + 0.001, ks + LAG["G"] + 0.001)

@@ -10,21 +10,19 @@ U8 = mybir.dt.uint8
 FP8X4 = mybir.dt.float8_e4m3fn_x4
 ALU = mybir.AluOpType
 FN = mybir.ActivationFunctionType
-AXIS = mybir.AxisListType
 
 P = 128
-B = 2048
-DIM = 256
+PACK = 4
+ROWS = 2048
 HID = 512
-D_OUT = 128
-TILES = B // P
-SIZES = [4,4,4,4]
-FLOPS = 2 * 2 * B * HID * (HID + D_OUT)
-PINNED = True
-
-LAG = {'hstep':0.01,'TW0':-6.44,'XW0':-2.21,'QW0':-0.88,'TW1':-1.59,'XW1':-0.21,'QW1':0.18,'TWO':0.62,'XWO':1.14,'QWO':1.34,'BMM':0.92,'XB':1.16,'T':-1.68,'X':-1.19,'QH':-0.55,'L1':-0.46,'RG':0.85,'QG':1.32,'L2':1.44,'G':0.61,'A':1.73,'TS':2.23,'EXP':2.8,'D':3.55,'E':2.56,'F':4.37,'LD':2.45,'LDX':2.86,'ET':3.31}
-RG_ON_ACT = []
-X_ON_DVE = []
+HALF = 128
+TILES = ROWS // P
+GROUP = 4
+COLS = GROUP * P
+UNITS = 2 * TILES // GROUP
+WORDS = HID // 2
+CLAMP = 2.0
+FLOPS = 2 * 2 * ROWS * HID * (HID + HALF)
 
 
 def tile_affinecouplinglayer_pa_kernel(
@@ -36,17 +34,14 @@ def tile_affinecouplinglayer_pa_kernel(
     b1_in = (s_bhid1, t_bhid1)
     wo_in = (s_Wout, t_Wout)
     bo_in = (s_bout, t_bout)
-    starts = [sum(SIZES[:q]) for q in range(len(SIZES))]
-    units = [(n, q) for q in range(len(SIZES)) for n in range(2)]
 
     with ExitStack() as ctx:
         keep = ctx.enter_context(tc.tile_pool(name="keep", bufs=1))
         work = ctx.enter_context(tc.tile_pool(name="work", bufs=2))
-        tp = ctx.enter_context(tc.psum_pool(name="tp", bufs=3))
-        l1 = ctx.enter_context(tc.psum_pool(name="l1", bufs=3))
-        l2 = ctx.enter_context(tc.psum_pool(name="l2", bufs=1))
-        if PINNED:
-            ctx.enter_context(tc.manual_schedule())
+        small = ctx.enter_context(tc.psum_pool(name="small", bufs=3))
+        acc1 = ctx.enter_context(tc.psum_pool(name="acc1", bufs=3))
+        acc2 = ctx.enter_context(tc.psum_pool(name="acc2", bufs=1))
+        ctx.enter_context(tc.manual_schedule())
 
         ident = keep.tile([P, P], F32, name="ident")
         make_identity(nc, ident[:])
@@ -54,371 +49,364 @@ def tile_affinecouplinglayer_pa_kernel(
         warm_out = keep.tile([P, 1], F32, name="warm_out")
         nc.vector.memset(warm_in[:], 0.0)
         nc.scalar.activation(out=warm_out[:], in_=warm_in[:], func=FN.Exp)
-        ones = keep.tile([P, P], BF16, name="ones")
-        nc.vector.memset(ones[:], 1.0)
+        ones_bf = keep.tile([P, P], BF16, name="ones_bf")
+        nc.vector.memset(ones_bf[:], 1.0)
         ones_f = keep.tile([P, 2], F32, name="ones_f")
         nc.vector.memset(ones_f[:], 1.0)
-        brow = keep.tile([P, 2 * D_OUT], BF16, name="brow")
-        nc.vector.memset(brow[:], 0.0)
+        bias_rows = keep.tile([P, 2 * HALF], BF16, name="bias_rows")
+        nc.vector.memset(bias_rows[:], 0.0)
 
         h_view = [h_in[n].rearrange("(p i) k -> p i k", i=TILES) for n in range(2)]
         z_view = z.rearrange("(p i) d -> p i d", i=TILES)
-        zo_view = out_0.rearrange("(p i) d -> p i d", i=TILES)
+        z_out_view = out_0.rearrange("(p i) d -> p i d", i=TILES)
 
-        w1raw = [keep.tile([P, 4 * HID], BF16, name="w1raw%d" % n) for n in range(2)]
-        b1raw = [keep.tile([P, 4], BF16, name="b1raw%d" % n) for n in range(2)]
-        woraw = [keep.tile([P, HID], BF16, name="woraw%d" % n) for n in range(2)]
-        bsraw = keep.tile([P, 1], BF16, name="bsraw")
-        bscol = keep.tile([P, 1], F32, name="bscol")
-        hraw = [keep.tile([P, SIZES[q] * HID], BF16, name="hraw%d_%d" % (n, q)) for (n, q) in units]
-        zraw = [keep.tile([P, SIZES[q] * DIM], BF16, name="zraw%d" % q) for q in range(len(SIZES))]
+        w1_rows = [keep.tile([P, PACK * HID], BF16, name="w1_rows%d" % n) for n in range(2)]
+        b1_bf = [keep.tile([P, PACK], BF16, name="b1_bf%d" % n) for n in range(2)]
+        wo_rows = [keep.tile([P, HID], BF16, name="wo_rows%d" % n) for n in range(2)]
+        bs_bf = keep.tile([P, 1], BF16, name="bs_bf")
+        h_rows = [keep.tile([P, GROUP * HID], BF16, name="h_rows%d" % k) for k in range(UNITS)]
+        z_rows = [keep.tile([P, GROUP * 2 * HALF], BF16, name="z_rows%d" % g) for g in range(UNITS // 2)]
 
         def load_w1(n):
             nc.sync.dma_start(
-                out=w1raw[n][:].rearrange("m (t k) -> m t k", t=4),
-                in_=w1_in[n].rearrange("(m t) k -> m t k", t=4),
+                out=w1_rows[n][:].rearrange("m (t k) -> m t k", t=PACK),
+                in_=w1_in[n].rearrange("(m t) k -> m t k", t=PACK),
             )
 
         def load_b1(n):
-            nc.sync.dma_start(out=b1raw[n][:], in_=b1_in[n].rearrange("(m t) -> m t", t=4))
+            nc.sync.dma_start(out=b1_bf[n][:], in_=b1_in[n].rearrange("(m t) -> m t", t=PACK))
 
         def load_h(k):
-            n, q = units[k]
+            first = (k // 2) * GROUP
             nc.sync.dma_start(
-                out=hraw[k][:].rearrange("p (j k) -> p j k", j=SIZES[q]),
-                in_=h_view[n][:, starts[q] : starts[q] + SIZES[q], :],
+                out=h_rows[k][:].rearrange("p (j k) -> p j k", j=GROUP),
+                in_=h_view[k % 2][:, first : first + GROUP, :],
             )
 
-        def load_z(q):
+        def load_z(g):
             nc.sync.dma_start(
-                out=zraw[q][:].rearrange("p (j d) -> p j d", j=SIZES[q]),
-                in_=z_view[:, starts[q] : starts[q] + SIZES[q], :],
+                out=z_rows[g][:].rearrange("p (j d) -> p j d", j=GROUP),
+                in_=z_view[:, g * GROUP : (g + 1) * GROUP, :],
             )
 
-        load_w1(0)
-        load_h(0)
-        load_b1(0)
-        load_w1(1)
-        load_h(1)
-        load_b1(1)
         for n in range(2):
-            nc.sync.dma_start(out=woraw[n][:], in_=wo_in[n])
+            load_w1(n)
+            load_h(n)
+            load_b1(n)
+        for n in range(2):
+            nc.sync.dma_start(out=wo_rows[n][:], in_=wo_in[n])
         for n in range(2):
             nc.sync.dma_start(
-                out=brow[0:1, n * D_OUT : (n + 1) * D_OUT], in_=bo_in[n].rearrange("(o c) -> o c", o=1)
+                out=bias_rows[0:1, n * HALF : (n + 1) * HALF], in_=bo_in[n].rearrange("(o c) -> o c", o=1)
             )
-        nc.sync.dma_start(out=bsraw[:], in_=bo_in[0].rearrange("(o c) -> o c", c=1))
-        for q in range(1, len(SIZES)):
-            load_h(2 * q)
-            load_h(2 * q + 1)
-            load_z(q - 1)
-        load_z(len(SIZES) - 1)
+        nc.sync.dma_start(out=bs_bf[:], in_=bo_in[0].rearrange("(o c) -> o c", c=1))
+        for g in range(1, UNITS // 2):
+            load_h(2 * g)
+            load_h(2 * g + 1)
+            load_z(g - 1)
+        load_z(UNITS // 2 - 1)
 
-        def copy_out(engine, out, in_):
-            if engine == "act":
-                nc.scalar.copy(out=out, in_=in_)
-            else:
-                nc.vector.tensor_copy(out=out, in_=in_)
+        w1_grouped = [keep.tile([P, PACK * HID], BF16, name="w1_grouped%d" % n, align_bytes=64) for n in range(2)]
+        w1_codes = [keep.tile([P, HID], U32, name="w1_codes%d" % n, align_bytes=64) for n in range(2)]
+        w1_scales = [keep.tile([P, HID], U8, name="w1_scales%d" % n, align_bytes=64) for n in range(2)]
+        b1 = [keep.tile([P, PACK], F32, name="b1_%d" % n) for n in range(2)]
+        wo_grouped = keep.tile([P, 2 * HALF * PACK], BF16, name="wo_grouped", align_bytes=64)
+        wo_codes = keep.tile([P, 2 * HALF], U32, name="wo_codes", align_bytes=64)
+        wo_scales = keep.tile([P, 2 * HALF], U8, name="wo_scales", align_bytes=64)
+        bias_all = keep.tile([P, 2 * HALF], F32, name="bias_all")
+        bs = keep.tile([P, 1], F32, name="bs")
+        log_det = keep.tile([P, TILES], F32, name="log_det")
+        live = {}
 
-        def transposes(raw, first, count):
-            raw_w = raw[:].bitcast(F32)
-            bank = tp.tile([P, 512], F32, name="bank", tag="tp")
-            width = count * P
-            for jj in range(count):
-                j = first + jj
+        def is_unit(k):
+            return 0 <= k < UNITS
+
+        def is_s(k):
+            return is_unit(k) and k % 2 == 0
+
+        def is_t(k):
+            return is_unit(k) and k % 2 == 1
+
+        def transpose_words(rows, first):
+            words = rows[:].bitcast(F32)
+            bank = small.tile([P, COLS], F32, name="bank", tag="small")
+            for c in range(2):
                 for u in range(2):
                     nc.tensor.transpose(
-                        bank[:, u * width + jj * P : u * width + (jj + 1) * P],
-                        raw_w[:, j * 256 + u * P : j * 256 + (u + 1) * P],
+                        bank[:, (2 * u + c) * P : (2 * u + c + 1) * P],
+                        words[:, (first + c) * WORDS + u * P : (first + c) * WORDS + (u + 1) * P],
                         ident[:],
                     )
             return bank
 
-        def leave(engine, bank, grouped, first, count):
-            width = count * P
-            copy_out(
-                engine,
-                grouped[:].bitcast(F32)[:, first * 256 : (first + count) * 256].rearrange("p (c u) -> p c u", u=2),
-                bank[:, 0 : 2 * width].rearrange("p (u c) -> p c u", u=2),
+        def interleave(copy, bank, grouped, first):
+            copy(
+                out=grouped[:].bitcast(F32)[:, first * 2 * P : (first + 2) * 2 * P].rearrange("p (c u) -> p c u", u=2),
+                in_=bank[:].rearrange("p (u c) -> p c u", u=2),
             )
 
         def quantise(grouped, codes, scales):
             nc.vector.quantize_mx(out=codes[:].bitcast(FP8X4), scales=scales[:], in_=grouped[:])
 
-        w1g = [keep.tile([P, 4 * HID], BF16, name="w1g%d" % n, align_bytes=64) for n in range(2)]
-        w1q = [keep.tile([P, HID], U32, name="w1q%d" % n, align_bytes=64) for n in range(2)]
-        w1sc = [keep.tile([P, HID], U8, name="w1sc%d" % n, align_bytes=64) for n in range(2)]
-        b1f = [keep.tile([P, 4], F32, name="b1f%d" % n) for n in range(2)]
-        wog = keep.tile([P, 8 * D_OUT], BF16, name="wog", align_bytes=64)
-        woq = keep.tile([P, 2 * D_OUT], U32, name="woq", align_bytes=64)
-        wosc = keep.tile([P, 2 * D_OUT], U8, name="wosc", align_bytes=64)
-        bias_bc = keep.tile([P, 2 * D_OUT], F32, name="bias_bc")
-        ld = keep.tile([P, TILES], F32, name="ld")
-        st = {}
+        def by_tile(ap):
+            return ap.rearrange("p (j o) -> p j o", j=GROUP)
 
-        def TW(n, h):
-            st[("wb", n, h)] = transposes(w1raw[n], 2 * h, 2)
+        def z_half(tile, half):
+            return tile[:].rearrange("p (j d) -> p j d", j=GROUP)[:, :, half * HALF : (half + 1) * HALF]
 
-        def XW(n, h):
-            leave(("act", "dve")[h], st[("wb", n, h)], w1g[n], 2 * h, 2)
+        def w1_transposes(k):
+            if k in (0, 1):
+                live[("w1_bank", k)] = [transpose_words(w1_rows[k], first) for first in (0, 2)]
 
-        def QW(n):
-            quantise(w1g[n], w1q[n], w1sc[n])
-            nc.vector.tensor_copy(out=b1f[n][:], in_=b1raw[n][:])
+        def w1_copies(k):
+            if k in (0, 1):
+                interleave(nc.scalar.copy, live[("w1_bank", k)][0], w1_grouped[k], 0)
+                interleave(nc.vector.tensor_copy, live[("w1_bank", k)][1], w1_grouped[k], 2)
 
-        def TWO():
-            bank = tp.tile([P, 512], F32, name="bank", tag="tp")
-            for n in range(2):
-                words = woraw[n][:].bitcast(F32).rearrange("o (p u) -> o p u", u=2)
-                for u in range(2):
-                    nc.tensor.transpose(bank[:, u * 256 + n * P : u * 256 + (n + 1) * P], words[:, :, u], ident[:])
-            st["wob"] = bank
+        def w1_quantise(k):
+            if k in (0, 1):
+                quantise(w1_grouped[k], w1_codes[k], w1_scales[k])
+                nc.vector.tensor_copy(out=b1[k][:], in_=b1_bf[k][:])
 
-        def XWO():
-            leave("dve", st["wob"], wog, 0, 2)
+        def wout_transposes(k):
+            if k == 0:
+                bank = small.tile([P, COLS], F32, name="bank", tag="small")
+                for n in range(2):
+                    words = wo_rows[n][:].bitcast(F32).rearrange("o (p u) -> o p u", u=2)
+                    for u in range(2):
+                        nc.tensor.transpose(bank[:, (2 * u + n) * P : (2 * u + n + 1) * P], words[:, :, u], ident[:])
+                live["wo_bank"] = bank
 
-        def QWO():
-            quantise(wog, woq, wosc)
+        def wout_copy(k):
+            if k == 0:
+                interleave(nc.vector.tensor_copy, live["wo_bank"], wo_grouped, 0)
 
-        def BMM():
-            bank = tp.tile([P, 512], F32, name="bank", tag="tp")
-            nc.tensor.matmul(out=bank[:, 0 : 2 * D_OUT], lhsT=ones[:], rhs=brow[:], start=True, stop=True)
-            st["bb"] = bank
+        def wout_quantise(k):
+            if k == 0:
+                quantise(wo_grouped, wo_codes, wo_scales)
 
-        def XB():
-            copy_out("dve", bias_bc[:], st["bb"][:, 0 : 2 * D_OUT])
-            nc.vector.tensor_copy(out=bscol[:], in_=bsraw[:])
+        def bias_matmul(k):
+            if k == 0:
+                bank = small.tile([P, COLS], F32, name="bank", tag="small")
+                nc.tensor.matmul(out=bank[:, 0 : 2 * HALF], lhsT=ones_bf[:], rhs=bias_rows[:], start=True, stop=True)
+                live["bias_bank"] = bank
 
-        def size(k):
-            return SIZES[units[k][1]]
+        def bias_copies(k):
+            if k == 0:
+                nc.vector.tensor_copy(out=bias_all[:], in_=live["bias_bank"][:, 0 : 2 * HALF])
+                nc.vector.tensor_copy(out=bs[:], in_=bs_bf[:])
 
-        def T(k, h):
-            if h == 0:
-                st[("hg", k)] = work.tile([P, size(k) * HID], BF16, name="hg", tag="hg", align_bytes=64)
-            st[("tb", k, h)] = transposes(hraw[k], 2 * h, min(2, size(k) - 2 * h))
+        def h_transposes(k):
+            if is_unit(k):
+                live[("h_grouped", k)] = work.tile([P, COLS * PACK], BF16, name="h_grouped", tag="h_grouped", align_bytes=64)
+                live[("h_bank", k)] = [transpose_words(h_rows[k], first) for first in (0, 2)]
 
-        def X(k, h):
-            engine = "dve" if [k, h] in X_ON_DVE else "act"
-            leave(engine, st[("tb", k, h)], st[("hg", k)], 2 * h, min(2, size(k) - 2 * h))
+        def h_copies(k):
+            if is_unit(k):
+                for half in range(2):
+                    interleave(nc.scalar.copy, live[("h_bank", k)][half], live[("h_grouped", k)], 2 * half)
 
-        def QH(k):
-            cols = size(k) * P
-            codes = work.tile([P, cols], U32, name="hq", tag="hq", bufs=3, align_bytes=64)
-            scales = work.tile([P, cols], U8, name="hsc", tag="hsc", bufs=3, align_bytes=64)
-            quantise(st[("hg", k)], codes, scales)
-            st[("hq", k)] = (codes, scales)
+        def h_quantise(k):
+            if is_unit(k):
+                codes = work.tile([P, COLS], U32, name="h_codes", tag="h_codes", bufs=3, align_bytes=64)
+                scales = work.tile([P, COLS], U8, name="h_scales", tag="h_scales", bufs=3, align_bytes=64)
+                quantise(live[("h_grouped", k)], codes, scales)
+                live[("h_codes", k)] = (codes, scales)
 
-        def L1(k, t):
-            n = units[k][0]
-            cols = size(k) * P
-            per = 512 // cols
-            if t % per == 0:
-                st[("acc", k, t // per)] = l1.tile([P, 512], F32, name="acc", tag="l1")
-            acc = st[("acc", k, t // per)]
-            codes, scales = st[("hq", k)]
-            nc.tensor.matmul_mx(
-                out=acc[:, (t % per) * cols : (t % per + 1) * cols],
-                lhsT=w1q[n][:, t * P : (t + 1) * P].bitcast(FP8X4),
-                lhsT_scale=w1sc[n][:, t * P : (t + 1) * P],
-                rhs=codes[:].bitcast(FP8X4),
-                rhs_scale=scales[:],
-                start=True,
-                stop=True,
-            )
-
-        def R(k, t):
-            n = units[k][0]
-            cols = size(k) * P
-            per = 512 // cols
-            if t == 0:
-                st[("gc", k)] = work.tile([P, 4 * cols], BF16, name="gc", tag="gc")
-            nc.scalar.activation(
-                out=st[("gc", k)][:, t * cols : (t + 1) * cols],
-                in_=st[("acc", k, t // per)][:, (t % per) * cols : (t % per + 1) * cols],
-                func=FN.Relu,
-                bias=b1f[n][:, t : t + 1],
-            )
-
-        def RG(k):
-            cols = size(k) * P
-            gg = work.tile([P, cols * 4], BF16, name="gg", tag="gg", align_bytes=64)
-            copy_out(
-                "act" if k in RG_ON_ACT else "dve",
-                gg[:].rearrange("p (c i t) -> p c t i", i=4, t=4),
-                st[("gc", k)][:].rearrange("p (t c i) -> p c t i", t=4, i=4),
-            )
-            st[("gg", k)] = gg
-
-        def QG(k):
-            cols = size(k) * P
-            codes = work.tile([P, cols], U32, name="gq", tag="gq", align_bytes=64)
-            scales = work.tile([P, cols], U8, name="gsc", tag="gsc", align_bytes=64)
-            quantise(st[("gg", k)], codes, scales)
-            st[("gq", k)] = (codes, scales)
-
-        def L2(k):
-            n = units[k][0]
-            codes, scales = st[("gq", k)]
-            o = l2.tile([P, 512], F32, name="o%d" % n, tag="o%d" % n)
-            st[("o", k)] = o
-            if n == 0:
+        def layer1(k, t):
+            if is_unit(k):
+                n = k % 2
+                codes, scales = live[("h_codes", k)]
+                acc = acc1.tile([P, COLS], F32, name="acc", tag="acc1")
                 nc.tensor.matmul_mx(
-                    out=o[:, 0 : size(k) * P],
-                    lhsT=woq[:, 0:P].bitcast(FP8X4),
-                    lhsT_scale=wosc[:, 0:P],
+                    out=acc[:],
+                    lhsT=w1_codes[n][:, t * P : (t + 1) * P].bitcast(FP8X4),
+                    lhsT_scale=w1_scales[n][:, t * P : (t + 1) * P],
                     rhs=codes[:].bitcast(FP8X4),
                     rhs_scale=scales[:],
                     start=True,
                     stop=True,
                 )
-                return
-            for j in range(size(k)):
+                live[("acc", k, t)] = acc
+
+        def relu_out(k, t):
+            if is_unit(k):
+                if t == 0:
+                    live[("g", k)] = work.tile([P, PACK * COLS], BF16, name="g", tag="g")
+                nc.scalar.activation(
+                    out=live[("g", k)][:, t * COLS : (t + 1) * COLS],
+                    in_=live[("acc", k, t)][:],
+                    func=FN.Relu,
+                    bias=b1[k % 2][:, t : t + 1],
+                )
+
+        def regroup(k):
+            if is_unit(k):
+                grouped = work.tile([P, COLS * PACK], BF16, name="g_grouped", tag="g_grouped", align_bytes=64)
+                nc.vector.tensor_copy(
+                    out=grouped[:].rearrange("p (c i t) -> p c t i", i=4, t=PACK),
+                    in_=live[("g", k)][:].rearrange("p (t c i) -> p c t i", t=PACK, i=4),
+                )
+                live[("g_grouped", k)] = grouped
+
+        def g_quantise(k):
+            if is_unit(k):
+                codes = work.tile([P, COLS], U32, name="g_codes", tag="g_codes", align_bytes=64)
+                scales = work.tile([P, COLS], U8, name="g_scales", tag="g_scales", align_bytes=64)
+                quantise(live[("g_grouped", k)], codes, scales)
+                live[("g_codes", k)] = (codes, scales)
+
+        def layer2(k):
+            if is_s(k):
+                codes, scales = live[("g_codes", k)]
+                o = acc2.tile([P, COLS], F32, name="o_s", tag="o_s")
                 nc.tensor.matmul_mx(
-                    out=o[:, j * P : (j + 1) * P],
-                    lhsT=codes[:, j * P : (j + 1) * P].bitcast(FP8X4),
-                    lhsT_scale=scales[:, j * P : (j + 1) * P],
-                    rhs=woq[:, n * P : (n + 1) * P].bitcast(FP8X4),
-                    rhs_scale=wosc[:, n * P : (n + 1) * P],
+                    out=o[:],
+                    lhsT=wo_codes[:, 0:HALF].bitcast(FP8X4),
+                    lhsT_scale=wo_scales[:, 0:HALF],
+                    rhs=codes[:].bitcast(FP8X4),
+                    rhs_scale=scales[:],
                     start=True,
                     stop=True,
                 )
-            st[("o", k)] = o
+                live[("o", k)] = o
+            if is_t(k):
+                codes, scales = live[("g_codes", k)]
+                o = acc2.tile([P, COLS], F32, name="o_t", tag="o_t")
+                for j in range(GROUP):
+                    nc.tensor.matmul_mx(
+                        out=o[:, j * P : (j + 1) * P],
+                        lhsT=codes[:, j * P : (j + 1) * P].bitcast(FP8X4),
+                        lhsT_scale=scales[:, j * P : (j + 1) * P],
+                        rhs=wo_codes[:, HALF : 2 * HALF].bitcast(FP8X4),
+                        rhs_scale=wo_scales[:, HALF : 2 * HALF],
+                        start=True,
+                        stop=True,
+                    )
+                live[("o", k)] = o
 
-        def by_tile(ap, q):
-            return ap.rearrange("p (j o) -> p j o", j=SIZES[q])
-
-        def bias_view(n, q):
-            return bias_bc[:, n * D_OUT : (n + 1) * D_OUT].unsqueeze(1).to_broadcast([P, SIZES[q], D_OUT])
-
-        def ep_tile(name, q):
-            return work.tile([P, SIZES[q] * D_OUT], F32, name=name, tag=name)
-
-        def G(q):
-            zo = work.tile([P, SIZES[q] * DIM], F32, name="zo", tag="zo", bufs=4)
-            st[("zo", q)] = zo
-            nc.gpsimd.tensor_scalar(
-                out=zo[:].rearrange("p (j d) -> p j d", j=SIZES[q])[:, :, 0:D_OUT],
-                in0=zraw[q][:].rearrange("p (j d) -> p j d", j=SIZES[q])[:, :, 0:D_OUT],
-                scalar1=1.0,
-                scalar2=0.0,
-                op0=ALU.mult,
-                op1=ALU.add,
-            )
-
-        def A(q):
-            a = ep_tile("a", q)
-            nc.vector.tensor_scalar(
-                out=a[:], in0=st[("o", 2 * q)][:, 0 : SIZES[q] * D_OUT], scalar1=bscol[:, 0:1], scalar2=2.0, op0=ALU.add, op1=ALU.min
-            )
-            st[("a", q)] = a
-
-        def TS(q):
-            ls = ep_tile("ls", q)
-            nc.vector.tensor_scalar_max(out=ls[:], in0=st[("a", q)][:], scalar1=-2.0)
-            st[("ls", q)] = ls
-
-        def EXP(q):
-            e = ep_tile("e", q)
-            nc.scalar.activation(out=e[:], in_=st[("ls", q)][:], func=FN.Exp)
-            st[("e", q)] = e
-
-        def LD(q):
-            bank = tp.tile([P, 512], F32, name="bank", tag="tp")
-            for j in range(SIZES[q]):
-                nc.tensor.matmul(
-                    out=bank[:, 2 * j : 2 * j + 2],
-                    lhsT=st[("ls", q)][:, j * P : (j + 1) * P],
-                    rhs=ones_f[:],
-                    start=True,
-                    stop=True,
+        def bias_clamp_high(k):
+            if is_s(k):
+                capped = work.tile([P, COLS], F32, name="capped", tag="capped")
+                nc.vector.tensor_scalar(
+                    out=capped[:], in0=live[("o", k)][:], scalar1=bs[:, 0:1], scalar2=CLAMP, op0=ALU.add, op1=ALU.min
                 )
-            st[("ldb", q)] = bank
+                live[("capped", k)] = capped
 
-        def LDX(q):
-            nc.vector.tensor_copy(
-                out=ld[:, starts[q] : starts[q] + SIZES[q]],
-                in_=st[("ldb", q)][:, 0 : 2 * SIZES[q]].rearrange("p (j c) -> p j c", c=2)[:, :, 0],
-            )
+        def clamp_low(k):
+            if is_s(k):
+                log_s = work.tile([P, COLS], F32, name="log_s", tag="log_s")
+                nc.vector.tensor_scalar_max(out=log_s[:], in0=live[("capped", k)][:], scalar1=-CLAMP)
+                live[("log_s", k)] = log_s
 
-        def ET(q):
-            bank = tp.tile([P, 512], F32, name="bank", tag="tp")
-            for j in range(SIZES[q]):
-                nc.tensor.transpose(bank[:, j * P : (j + 1) * P], st[("e", q)][:, j * P : (j + 1) * P], ident[:])
-            st[("eb", q)] = bank
+        def exp(k):
+            if is_s(k):
+                scale = work.tile([P, COLS], F32, name="scale", tag="scale")
+                nc.scalar.activation(out=scale[:], in_=live[("log_s", k)][:], func=FN.Exp)
+                live[("scale", k)] = scale
 
-        def D(q):
-            m = ep_tile("m", q)
-            nc.vector.tensor_tensor(
-                out=by_tile(m[:], q),
-                in0=by_tile(st[("eb", q)][:, 0 : SIZES[q] * D_OUT], q),
-                in1=zraw[q][:].rearrange("p (j d) -> p j d", j=SIZES[q])[:, :, D_OUT:DIM],
-                op=ALU.mult,
-            )
-            st[("m", q)] = m
+        def row_sums(k):
+            if is_s(k):
+                bank = small.tile([P, COLS], F32, name="bank", tag="small")
+                for j in range(GROUP):
+                    nc.tensor.matmul(
+                        out=bank[:, 2 * j : 2 * j + 2],
+                        lhsT=live[("log_s", k)][:, j * P : (j + 1) * P],
+                        rhs=ones_f[:],
+                        start=True,
+                        stop=True,
+                    )
+                live[("sum_bank", k)] = bank
 
-        def E(q):
-            r = ep_tile("r", q)
-            nc.vector.tensor_tensor(
-                out=by_tile(r[:], q), in0=by_tile(st[("o", 2 * q + 1)][:, 0 : SIZES[q] * D_OUT], q), in1=bias_view(1, q), op=ALU.add
-            )
-            st[("r", q)] = r
+        def row_sums_copy(k):
+            if is_s(k):
+                first = (k // 2) * GROUP
+                nc.vector.tensor_copy(
+                    out=log_det[:, first : first + GROUP],
+                    in_=live[("sum_bank", k)][:, 0 : 2 * GROUP].rearrange("p (j c) -> p j c", c=2)[:, :, 0],
+                )
 
-        def F(q):
-            nc.vector.tensor_tensor(
-                out=st[("zo", q)][:].rearrange("p (j d) -> p j d", j=SIZES[q])[:, :, D_OUT:DIM],
-                in0=by_tile(st[("r", q)][:], q),
-                in1=by_tile(st[("m", q)][:], q),
-                op=ALU.add,
-            )
+        def exp_back(k):
+            if is_s(k):
+                bank = small.tile([P, COLS], F32, name="bank", tag="small")
+                for j in range(GROUP):
+                    nc.tensor.transpose(
+                        bank[:, j * P : (j + 1) * P], live[("scale", k)][:, j * P : (j + 1) * P], ident[:]
+                    )
+                live[("scale_bank", k)] = bank
 
-        def ST(q):
-            nc.sync.dma_start(
-                out=zo_view[:, starts[q] : starts[q] + SIZES[q], :],
-                in_=st[("zo", q)][:].rearrange("p (j d) -> p j d", j=SIZES[q]),
-            )
+        def times_z2(k):
+            if is_s(k):
+                scaled = work.tile([P, COLS], F32, name="scaled", tag="scaled")
+                nc.vector.tensor_tensor(
+                    out=by_tile(scaled[:]), in0=by_tile(live[("scale_bank", k)][:]), in1=z_half(z_rows[k // 2], 1), op=ALU.mult
+                )
+                live[("scaled", k)] = scaled
 
-        plan = []
+        def cast_z1(k):
+            if is_s(k):
+                z_out = work.tile([P, GROUP * 2 * HALF], F32, name="z_out", tag="z_out", bufs=UNITS // 2)
+                nc.gpsimd.tensor_scalar(
+                    out=z_half(z_out, 0), in0=z_half(z_rows[k // 2], 0), scalar1=1.0, scalar2=0.0, op0=ALU.mult, op1=ALU.add
+                )
+                live[("z_out", k // 2)] = z_out
 
-        def at(position, fn, *args):
-            plan.append((position, len(plan), fn, args))
+        def shift_bias(k):
+            if is_t(k):
+                shift = work.tile([P, COLS], F32, name="shift", tag="shift")
+                nc.vector.tensor_tensor(
+                    out=by_tile(shift[:]),
+                    in0=by_tile(live[("o", k)][:]),
+                    in1=bias_all[:, HALF : 2 * HALF].unsqueeze(1).to_broadcast([P, GROUP, HALF]),
+                    op=ALU.add,
+                )
+                live[("shift", k)] = shift
 
-        step = LAG["hstep"]
-        for n in range(2):
-            for h in range(2):
-                at(LAG["TW%d" % n] + h * step, TW, n, h)
-                at(LAG["XW%d" % n] + h * step, XW, n, h)
-            at(LAG["QW%d" % n], QW, n)
-        at(LAG["TWO"], TWO)
-        at(LAG["XWO"], XWO)
-        at(LAG["QWO"], QWO)
-        at(LAG["BMM"], BMM)
-        at(LAG["XB"], XB)
-        for k in range(len(units)):
-            for h in range((size(k) + 1) // 2):
-                at(k + LAG["T"] + h * step, T, k, h)
-                at(k + LAG["X"] + h * step, X, k, h)
-            at(k + LAG["QH"], QH, k)
-            for t in range(4):
-                at(k + LAG["L1"] + t * 0.25, L1, k, t)
-                at(k + t * 0.25, R, k, t)
-            at(k + LAG["RG"], RG, k)
-            at(k + LAG["QG"], QG, k)
-            at(k + LAG["L2"], L2, k)
-        for q in range(len(SIZES)):
-            ks = 2 * q
-            kt = 2 * q + 1
-            at(ks + LAG["G"], G, q)
-            at(ks + LAG["A"], A, q)
-            at(ks + LAG["TS"], TS, q)
-            at(ks + LAG["EXP"], EXP, q)
-            at(ks + LAG["LD"], LD, q)
-            at(ks + LAG["LDX"], LDX, q)
-            at(ks + LAG["ET"], ET, q)
-            at(ks + LAG["D"], D, q)
-            at(kt + LAG["E"], E, q)
-            last = max(kt + LAG["F"], ks + LAG["D"] + 0.001, ks + LAG["G"] + 0.001)
-            at(last, F, q)
-            at(last + 0.001, ST, q)
-        for entry in sorted(plan, key=lambda e: (e[0], e[1])):
-            entry[2](*entry[3])
-        nc.sync.dma_start(out=out_1.rearrange("(p i) -> p i", i=TILES), in_=ld[:])
+        def add_and_store(k):
+            if is_t(k):
+                g = k // 2
+                nc.vector.tensor_tensor(
+                    out=z_half(live[("z_out", g)], 1),
+                    in0=by_tile(live[("shift", k)][:]),
+                    in1=by_tile(live[("scaled", k - 1)][:]),
+                    op=ALU.add,
+                )
+                nc.sync.dma_start(
+                    out=z_out_view[:, g * GROUP : (g + 1) * GROUP, :],
+                    in_=live[("z_out", g)][:].rearrange("p (j d) -> p j d", j=GROUP),
+                )
+
+        for i in range(-3, UNITS + 4):
+            relu_out(i, 0)
+            layer1(i, 2)
+            wout_copy(i - 1)
+            bias_copies(i - 1)
+            w1_quantise(i + 1)
+            clamp_low(i - 2)
+            relu_out(i, 1)
+            layer1(i, 3)
+            exp_back(i - 4)
+            h_transposes(i + 2)
+            add_and_store(i - 4)
+            g_quantise(i - 1)
+            wout_quantise(i - 1)
+            w1_transposes(i + 3)
+            layer2(i - 1)
+            h_quantise(i + 1)
+            row_sums(i - 3)
+            relu_out(i, 2)
+            layer1(i + 1, 0)
+            times_z2(i - 4)
+            shift_bias(i - 2)
+            cast_z1(i)
+            wout_transposes(i)
+            bias_clamp_high(i - 1)
+            relu_out(i, 3)
+            layer1(i + 1, 1)
+            w1_copies(i + 2)
+            exp(i - 2)
+            h_copies(i + 2)
+            regroup(i)
+            row_sums_copy(i - 3)
+            bias_matmul(i)
+        nc.sync.dma_start(out=out_1.rearrange("(p i) -> p i", i=TILES), in_=log_det[:])

@@ -61,27 +61,27 @@ def tile_affinecouplinglayer_pa_kernel(
         z_out_view = out_0.rearrange("(p i) d -> p i d", i=TILES)
 
         w1_rows = [keep.tile([P, PACK * HID], BF16, name="w1_rows%d" % n) for n in range(2)]
-        b1_bf = [keep.tile([P, PACK], BF16, name="b1_bf%d" % n) for n in range(2)]
+        b1 = [keep.tile([P, PACK], BF16, name="b1_%d" % n) for n in range(2)]
         wo_rows = [keep.tile([P, HID], BF16, name="wo_rows%d" % n) for n in range(2)]
-        bs_bf = keep.tile([P, 1], BF16, name="bs_bf")
+        bs = keep.tile([P, 1], BF16, name="bs")
         h_rows = [keep.tile([P, GROUP * HID], BF16, name="h_rows%d" % k) for k in range(UNITS)]
         z_rows = [keep.tile([P, GROUP * 2 * HALF], BF16, name="z_rows%d" % g) for g in range(UNITS // 2)]
 
         def load_w1(n):
-            nc.sync.dma_start(
-                out=w1_rows[n][:].rearrange("m (t k) -> m t k", t=PACK),
-                in_=w1_in[n].rearrange("(m t) k -> m t k", t=PACK),
-            )
+            for first in (0, 2):
+                nc.sync.dma_start(
+                    out=w1_rows[n][:].rearrange("m (t k) -> m t k", t=PACK)[:, first : first + 2, :],
+                    in_=w1_in[n].rearrange("(m t) k -> m t k", t=PACK)[:, first : first + 2, :],
+                )
 
-        def load_b1(n):
-            nc.sync.dma_start(out=b1_bf[n][:], in_=b1_in[n].rearrange("(m t) -> m t", t=PACK))
 
         def load_h(k):
-            first = (k // 2) * GROUP
-            nc.sync.dma_start(
-                out=h_rows[k][:].rearrange("p (j k) -> p j k", j=GROUP),
-                in_=h_view[k % 2][:, first : first + GROUP, :],
-            )
+            for first in (0, 2):
+                tile_0 = (k // 2) * GROUP + first
+                nc.sync.dma_start(
+                    out=h_rows[k][:].rearrange("p (j k) -> p j k", j=GROUP)[:, first : first + 2, :],
+                    in_=h_view[k % 2][:, tile_0 : tile_0 + 2, :],
+                )
 
         def load_z(g):
             nc.sync.dma_start(
@@ -90,16 +90,17 @@ def tile_affinecouplinglayer_pa_kernel(
             )
 
         for n in range(2):
-            load_w1(n)
-            load_h(n)
-            load_b1(n)
+            nc.scalar.dma_start(out=b1[n][:], in_=b1_in[n].rearrange("(m t) -> m t", t=PACK))
         for n in range(2):
-            nc.sync.dma_start(out=wo_rows[n][:], in_=wo_in[n])
-        for n in range(2):
-            nc.sync.dma_start(
+            nc.scalar.dma_start(
                 out=bias_rows[0:1, n * HALF : (n + 1) * HALF], in_=bo_in[n].rearrange("(o c) -> o c", o=1)
             )
-        nc.sync.dma_start(out=bs_bf[:], in_=bo_in[0].rearrange("(o c) -> o c", c=1))
+        nc.scalar.dma_start(out=bs[:], in_=bo_in[0].rearrange("(o c) -> o c", c=1))
+        for n in range(2):
+            load_w1(n)
+            load_h(n)
+        for n in range(2):
+            nc.sync.dma_start(out=wo_rows[n][:], in_=wo_in[n])
         for g in range(1, UNITS // 2):
             load_h(2 * g)
             load_h(2 * g + 1)
@@ -109,12 +110,10 @@ def tile_affinecouplinglayer_pa_kernel(
         w1_grouped = [keep.tile([P, PACK * HID], BF16, name="w1_grouped%d" % n, align_bytes=64) for n in range(2)]
         w1_codes = [keep.tile([P, HID], U32, name="w1_codes%d" % n, align_bytes=64) for n in range(2)]
         w1_scales = [keep.tile([P, HID], U8, name="w1_scales%d" % n, align_bytes=64) for n in range(2)]
-        b1 = [keep.tile([P, PACK], F32, name="b1_%d" % n) for n in range(2)]
         wo_grouped = keep.tile([P, 2 * HALF * PACK], BF16, name="wo_grouped", align_bytes=64)
         wo_codes = keep.tile([P, 2 * HALF], U32, name="wo_codes", align_bytes=64)
         wo_scales = keep.tile([P, 2 * HALF], U8, name="wo_scales", align_bytes=64)
         bias_all = keep.tile([P, 2 * HALF], F32, name="bias_all")
-        bs = keep.tile([P, 1], F32, name="bs")
         log_det = keep.tile([P, TILES], F32, name="log_det")
         live = {}
 
@@ -166,7 +165,6 @@ def tile_affinecouplinglayer_pa_kernel(
         def w1_quantise(k):
             if k in (0, 1):
                 quantise(w1_grouped[k], w1_codes[k], w1_scales[k])
-                nc.vector.tensor_copy(out=b1[k][:], in_=b1_bf[k][:])
 
         def wout_transposes(k):
             if k == 0:
@@ -191,10 +189,9 @@ def tile_affinecouplinglayer_pa_kernel(
                 nc.tensor.matmul(out=bank[:, 0 : 2 * HALF], lhsT=ones_bf[:], rhs=bias_rows[:], start=True, stop=True)
                 live["bias_bank"] = bank
 
-        def bias_copies(k):
+        def bias_copy(k):
             if k == 0:
                 nc.vector.tensor_copy(out=bias_all[:], in_=live["bias_bank"][:, 0 : 2 * HALF])
-                nc.vector.tensor_copy(out=bs[:], in_=bs_bf[:])
 
         def h_transposes(k):
             if is_unit(k):
@@ -380,7 +377,7 @@ def tile_affinecouplinglayer_pa_kernel(
             relu_out(i, 0)
             layer1(i, 2)
             wout_copy(i - 1)
-            bias_copies(i - 1)
+            bias_copy(i - 1)
             w1_quantise(i + 1)
             clamp_low(i - 2)
             relu_out(i, 1)

@@ -21,6 +21,7 @@ GROUP = 4
 COLS = GROUP * P
 UNITS = 2 * TILES // GROUP
 WORDS = HID // 2
+PAIRS = (0, 2)
 CLAMP = 2.0
 FLOPS = 2 * 2 * ROWS * HID * (HID + HALF)
 
@@ -33,7 +34,6 @@ def tile_affinecouplinglayer_pa_kernel(
     w1_in = (s_Whid1, t_Whid1)
     b1_in = (s_bhid1, t_bhid1)
     wo_in = (s_Wout, t_Wout)
-    bo_in = (s_bout, t_bout)
 
     with ExitStack() as ctx:
         keep = ctx.enter_context(tc.tile_pool(name="keep", bufs=1))
@@ -53,87 +53,79 @@ def tile_affinecouplinglayer_pa_kernel(
         nc.vector.memset(ones_bf[:], 1.0)
         ones_f = keep.tile([P, 2], F32, name="ones_f")
         nc.vector.memset(ones_f[:], 1.0)
-        bias_rows = keep.tile([P, 2 * HALF], BF16, name="bias_rows")
-        nc.vector.memset(bias_rows[:], 0.0)
+        bt_rows = keep.tile([P, HALF], BF16, name="bt_rows")
+        nc.vector.memset(bt_rows[:], 0.0)
 
         h_view = [h_in[n].rearrange("(p i) k -> p i k", i=TILES) for n in range(2)]
         z_view = z.rearrange("(p i) d -> p i d", i=TILES)
         z_out_view = out_0.rearrange("(p i) d -> p i d", i=TILES)
 
         w1_rows = [keep.tile([P, PACK * HID], BF16, name="w1_rows%d" % n) for n in range(2)]
-        b1 = [keep.tile([P, PACK], BF16, name="b1_%d" % n) for n in range(2)]
+        b1_bf = [keep.tile([P, PACK], BF16, name="b1_bf%d" % n) for n in range(2)]
         wo_rows = [keep.tile([P, HID], BF16, name="wo_rows%d" % n) for n in range(2)]
-        bs = keep.tile([P, 1], BF16, name="bs")
-        h_rows = [keep.tile([P, GROUP * HID], BF16, name="h_rows%d" % k) for k in range(UNITS)]
-        z_rows = [keep.tile([P, GROUP * 2 * HALF], BF16, name="z_rows%d" % g) for g in range(UNITS // 2)]
+        bs_bf = keep.tile([P, 1], BF16, name="bs_bf")
+        h_rows = [keep.tile([P, GROUP * HID], BF16, name="h_rows%d" % v) for v in range(UNITS)]
+        z_rows = [keep.tile([P, GROUP * 2 * HALF], BF16, name="z_rows%d" % grp) for grp in range(UNITS // 2)]
 
-        def load_w1(n):
-            for first in (0, 2):
-                nc.sync.dma_start(
-                    out=w1_rows[n][:].rearrange("m (t k) -> m t k", t=PACK)[:, first : first + 2, :],
-                    in_=w1_in[n].rearrange("(m t) k -> m t k", t=PACK)[:, first : first + 2, :],
-                )
-
-
-        def load_h(k):
-            for first in (0, 2):
-                tile_0 = (k // 2) * GROUP + first
-                nc.sync.dma_start(
-                    out=h_rows[k][:].rearrange("p (j k) -> p j k", j=GROUP)[:, first : first + 2, :],
-                    in_=h_view[k % 2][:, tile_0 : tile_0 + 2, :],
-                )
-
-        def load_z(g):
+        def load_h(v):
+            first = (v // 2) * GROUP
             nc.sync.dma_start(
-                out=z_rows[g][:].rearrange("p (j d) -> p j d", j=GROUP),
-                in_=z_view[:, g * GROUP : (g + 1) * GROUP, :],
+                out=h_rows[v][:].rearrange("p (j k) -> p j k", j=GROUP),
+                in_=h_view[v % 2][:, first : first + GROUP, :],
+            )
+
+        def load_z(grp):
+            nc.sync.dma_start(
+                out=z_rows[grp][:].rearrange("p (j d) -> p j d", j=GROUP),
+                in_=z_view[:, grp * GROUP : (grp + 1) * GROUP, :],
             )
 
         for n in range(2):
-            nc.scalar.dma_start(out=b1[n][:], in_=b1_in[n].rearrange("(m t) -> m t", t=PACK))
-        for n in range(2):
-            nc.scalar.dma_start(
-                out=bias_rows[0:1, n * HALF : (n + 1) * HALF], in_=bo_in[n].rearrange("(o c) -> o c", o=1)
+            nc.sync.dma_start(
+                out=w1_rows[n][:].rearrange("m (t k) -> m t k", t=PACK),
+                in_=w1_in[n].rearrange("(m t) k -> m t k", t=PACK),
             )
-        nc.scalar.dma_start(out=bs[:], in_=bo_in[0].rearrange("(o c) -> o c", c=1))
-        for n in range(2):
-            load_w1(n)
             load_h(n)
+            nc.sync.dma_start(out=b1_bf[n][:], in_=b1_in[n].rearrange("(m t) -> m t", t=PACK))
         for n in range(2):
             nc.sync.dma_start(out=wo_rows[n][:], in_=wo_in[n])
-        for g in range(1, UNITS // 2):
-            load_h(2 * g)
-            load_h(2 * g + 1)
-            load_z(g - 1)
+        nc.sync.dma_start(out=bt_rows[0:1, :], in_=t_bout.rearrange("(o c) -> o c", o=1))
+        nc.sync.dma_start(out=bs_bf[:], in_=s_bout.rearrange("(o c) -> o c", c=1))
+        for grp in range(1, UNITS // 2):
+            load_h(2 * grp)
+            load_h(2 * grp + 1)
+            load_z(grp - 1)
         load_z(UNITS // 2 - 1)
 
         w1_grouped = [keep.tile([P, PACK * HID], BF16, name="w1_grouped%d" % n, align_bytes=64) for n in range(2)]
         w1_codes = [keep.tile([P, HID], U32, name="w1_codes%d" % n, align_bytes=64) for n in range(2)]
         w1_scales = [keep.tile([P, HID], U8, name="w1_scales%d" % n, align_bytes=64) for n in range(2)]
+        b1 = [keep.tile([P, PACK], F32, name="b1_%d" % n) for n in range(2)]
         wo_grouped = keep.tile([P, 2 * HALF * PACK], BF16, name="wo_grouped", align_bytes=64)
         wo_codes = keep.tile([P, 2 * HALF], U32, name="wo_codes", align_bytes=64)
         wo_scales = keep.tile([P, 2 * HALF], U8, name="wo_scales", align_bytes=64)
-        bias_all = keep.tile([P, 2 * HALF], F32, name="bias_all")
+        bt_all = keep.tile([P, HALF], F32, name="bt_all")
+        bs = keep.tile([P, 1], F32, name="bs")
         log_det = keep.tile([P, TILES], F32, name="log_det")
         live = {}
 
-        def is_unit(k):
-            return 0 <= k < UNITS
+        def is_unit(v):
+            return 0 <= v < UNITS
 
-        def is_s(k):
-            return is_unit(k) and k % 2 == 0
+        def is_s(v):
+            return is_unit(v) and v % 2 == 0
 
-        def is_t(k):
-            return is_unit(k) and k % 2 == 1
+        def is_t(v):
+            return is_unit(v) and v % 2 == 1
 
         def transpose_words(rows, first):
             words = rows[:].bitcast(F32)
             bank = small.tile([P, COLS], F32, name="bank", tag="small")
-            for c in range(2):
+            for j in range(2):
                 for u in range(2):
                     nc.tensor.transpose(
-                        bank[:, (2 * u + c) * P : (2 * u + c + 1) * P],
-                        words[:, (first + c) * WORDS + u * P : (first + c) * WORDS + (u + 1) * P],
+                        bank[:, (2 * u + j) * P : (2 * u + j + 1) * P],
+                        words[:, (first + j) * WORDS + u * P : (first + j) * WORDS + (u + 1) * P],
                         ident[:],
                     )
             return bank
@@ -148,72 +140,74 @@ def tile_affinecouplinglayer_pa_kernel(
             nc.vector.quantize_mx(out=codes[:].bitcast(FP8X4), scales=scales[:], in_=grouped[:])
 
         def by_tile(ap):
-            return ap.rearrange("p (j o) -> p j o", j=GROUP)
+            return ap.rearrange("p (j c) -> p j c", j=GROUP)
 
-        def z_half(tile, half):
-            return tile[:].rearrange("p (j d) -> p j d", j=GROUP)[:, :, half * HALF : (half + 1) * HALF]
+        def z_part(z_tile, part):
+            return z_tile[:].rearrange("p (j d) -> p j d", j=GROUP)[:, :, part * HALF : (part + 1) * HALF]
 
-        def w1_transposes(k):
-            if k in (0, 1):
-                live[("w1_bank", k)] = [transpose_words(w1_rows[k], first) for first in (0, 2)]
+        def w1_transposes(v):
+            if v in (0, 1):
+                live[("w1_bank", v)] = [transpose_words(w1_rows[v], first) for first in PAIRS]
 
-        def w1_copies(k):
-            if k in (0, 1):
-                interleave(nc.scalar.copy, live[("w1_bank", k)][0], w1_grouped[k], 0)
-                interleave(nc.vector.tensor_copy, live[("w1_bank", k)][1], w1_grouped[k], 2)
+        def w1_copies(v):
+            if v in (0, 1):
+                interleave(nc.scalar.copy, live[("w1_bank", v)][0], w1_grouped[v], PAIRS[0])
+                interleave(nc.vector.tensor_copy, live[("w1_bank", v)][1], w1_grouped[v], PAIRS[1])
 
-        def w1_quantise(k):
-            if k in (0, 1):
-                quantise(w1_grouped[k], w1_codes[k], w1_scales[k])
+        def w1_quantise(v):
+            if v in (0, 1):
+                quantise(w1_grouped[v], w1_codes[v], w1_scales[v])
+                nc.vector.tensor_copy(out=b1[v][:], in_=b1_bf[v][:])
 
-        def wout_transposes(k):
-            if k == 0:
+        def wout_transposes(v):
+            if v == 0:
                 bank = small.tile([P, COLS], F32, name="bank", tag="small")
                 for n in range(2):
-                    words = wo_rows[n][:].bitcast(F32).rearrange("o (p u) -> o p u", u=2)
+                    words = wo_rows[n][:].bitcast(F32).rearrange("c (p u) -> c p u", u=2)
                     for u in range(2):
                         nc.tensor.transpose(bank[:, (2 * u + n) * P : (2 * u + n + 1) * P], words[:, :, u], ident[:])
                 live["wo_bank"] = bank
 
-        def wout_copy(k):
-            if k == 0:
+        def wout_copy(v):
+            if v == 0:
                 interleave(nc.vector.tensor_copy, live["wo_bank"], wo_grouped, 0)
 
-        def wout_quantise(k):
-            if k == 0:
+        def wout_quantise(v):
+            if v == 0:
                 quantise(wo_grouped, wo_codes, wo_scales)
 
-        def bias_matmul(k):
-            if k == 0:
+        def bias_matmul(v):
+            if v == 0:
                 bank = small.tile([P, COLS], F32, name="bank", tag="small")
-                nc.tensor.matmul(out=bank[:, 0 : 2 * HALF], lhsT=ones_bf[:], rhs=bias_rows[:], start=True, stop=True)
-                live["bias_bank"] = bank
+                nc.tensor.matmul(out=bank[:, 0:HALF], lhsT=ones_bf[:], rhs=bt_rows[:], start=True, stop=True)
+                live["bt_bank"] = bank
 
-        def bias_copy(k):
-            if k == 0:
-                nc.vector.tensor_copy(out=bias_all[:], in_=live["bias_bank"][:, 0 : 2 * HALF])
+        def bias_copies(v):
+            if v == 0:
+                nc.vector.tensor_copy(out=bt_all[:], in_=live["bt_bank"][:, 0:HALF])
+                nc.vector.tensor_copy(out=bs[:], in_=bs_bf[:])
 
-        def h_transposes(k):
-            if is_unit(k):
-                live[("h_grouped", k)] = work.tile([P, COLS * PACK], BF16, name="h_grouped", tag="h_grouped", align_bytes=64)
-                live[("h_bank", k)] = [transpose_words(h_rows[k], first) for first in (0, 2)]
+        def h_transposes(v):
+            if is_unit(v):
+                live[("h_grouped", v)] = work.tile([P, COLS * PACK], BF16, name="h_grouped", tag="h_grouped", align_bytes=64)
+                live[("h_bank", v)] = [transpose_words(h_rows[v], first) for first in PAIRS]
 
-        def h_copies(k):
-            if is_unit(k):
-                for half in range(2):
-                    interleave(nc.scalar.copy, live[("h_bank", k)][half], live[("h_grouped", k)], 2 * half)
+        def h_copies(v):
+            if is_unit(v):
+                for pair in range(2):
+                    interleave(nc.scalar.copy, live[("h_bank", v)][pair], live[("h_grouped", v)], PAIRS[pair])
 
-        def h_quantise(k):
-            if is_unit(k):
+        def h_quantise(v):
+            if is_unit(v):
                 codes = work.tile([P, COLS], U32, name="h_codes", tag="h_codes", bufs=3, align_bytes=64)
                 scales = work.tile([P, COLS], U8, name="h_scales", tag="h_scales", bufs=3, align_bytes=64)
-                quantise(live[("h_grouped", k)], codes, scales)
-                live[("h_codes", k)] = (codes, scales)
+                quantise(live[("h_grouped", v)], codes, scales)
+                live[("h_codes", v)] = (codes, scales)
 
-        def layer1(k, t):
-            if is_unit(k):
-                n = k % 2
-                codes, scales = live[("h_codes", k)]
+        def layer1(v, t):
+            if is_unit(v):
+                n = v % 2
+                codes, scales = live[("h_codes", v)]
                 acc = acc1.tile([P, COLS], F32, name="acc", tag="acc1")
                 nc.tensor.matmul_mx(
                     out=acc[:],
@@ -224,41 +218,41 @@ def tile_affinecouplinglayer_pa_kernel(
                     start=True,
                     stop=True,
                 )
-                live[("acc", k, t)] = acc
+                live[("acc", v, t)] = acc
 
-        def relu_out(k, t):
-            if is_unit(k):
+        def relu_out(v, t):
+            if is_unit(v):
                 if t == 0:
-                    live[("g", k)] = work.tile([P, PACK * COLS], BF16, name="g", tag="g")
+                    live[("g", v)] = work.tile([P, PACK * COLS], BF16, name="g", tag="g")
                 nc.scalar.activation(
-                    out=live[("g", k)][:, t * COLS : (t + 1) * COLS],
-                    in_=live[("acc", k, t)][:],
+                    out=live[("g", v)][:, t * COLS : (t + 1) * COLS],
+                    in_=live[("acc", v, t)][:],
                     func=FN.Relu,
-                    bias=b1[k % 2][:, t : t + 1],
+                    bias=b1[v % 2][:, t : t + 1],
                 )
 
-        def regroup(k):
-            if is_unit(k):
+        def regroup(v):
+            if is_unit(v):
                 grouped = work.tile([P, COLS * PACK], BF16, name="g_grouped", tag="g_grouped", align_bytes=64)
                 nc.vector.tensor_copy(
-                    out=grouped[:].rearrange("p (c i t) -> p c t i", i=4, t=PACK),
-                    in_=live[("g", k)][:].rearrange("p (t c i) -> p c t i", t=PACK, i=4),
+                    out=grouped[:].rearrange("p (c r t) -> p c t r", r=4, t=PACK),
+                    in_=live[("g", v)][:].rearrange("p (t c r) -> p c t r", t=PACK, r=4),
                 )
-                live[("g_grouped", k)] = grouped
+                live[("g_grouped", v)] = grouped
 
-        def g_quantise(k):
-            if is_unit(k):
+        def g_quantise(v):
+            if is_unit(v):
                 codes = work.tile([P, COLS], U32, name="g_codes", tag="g_codes", align_bytes=64)
                 scales = work.tile([P, COLS], U8, name="g_scales", tag="g_scales", align_bytes=64)
-                quantise(live[("g_grouped", k)], codes, scales)
-                live[("g_codes", k)] = (codes, scales)
+                quantise(live[("g_grouped", v)], codes, scales)
+                live[("g_codes", v)] = (codes, scales)
 
-        def layer2(k):
-            if is_s(k):
-                codes, scales = live[("g_codes", k)]
-                o = acc2.tile([P, COLS], F32, name="o_s", tag="o_s")
+        def layer2(v):
+            if is_s(v):
+                codes, scales = live[("g_codes", v)]
+                product = acc2.tile([P, COLS], F32, name="o_s", tag="o_s")
                 nc.tensor.matmul_mx(
-                    out=o[:],
+                    out=product[:],
                     lhsT=wo_codes[:, 0:HALF].bitcast(FP8X4),
                     lhsT_scale=wo_scales[:, 0:HALF],
                     rhs=codes[:].bitcast(FP8X4),
@@ -266,13 +260,13 @@ def tile_affinecouplinglayer_pa_kernel(
                     start=True,
                     stop=True,
                 )
-                live[("o", k)] = o
-            if is_t(k):
-                codes, scales = live[("g_codes", k)]
-                o = acc2.tile([P, COLS], F32, name="o_t", tag="o_t")
+                live[("o", v)] = product
+            if is_t(v):
+                codes, scales = live[("g_codes", v)]
+                product = acc2.tile([P, COLS], F32, name="o_t", tag="o_t")
                 for j in range(GROUP):
                     nc.tensor.matmul_mx(
-                        out=o[:, j * P : (j + 1) * P],
+                        out=product[:, j * P : (j + 1) * P],
                         lhsT=codes[:, j * P : (j + 1) * P].bitcast(FP8X4),
                         lhsT_scale=scales[:, j * P : (j + 1) * P],
                         rhs=wo_codes[:, HALF : 2 * HALF].bitcast(FP8X4),
@@ -280,104 +274,104 @@ def tile_affinecouplinglayer_pa_kernel(
                         start=True,
                         stop=True,
                     )
-                live[("o", k)] = o
+                live[("o", v)] = product
 
-        def bias_clamp_high(k):
-            if is_s(k):
+        def bias_clamp_high(v):
+            if is_s(v):
                 capped = work.tile([P, COLS], F32, name="capped", tag="capped")
                 nc.vector.tensor_scalar(
-                    out=capped[:], in0=live[("o", k)][:], scalar1=bs[:, 0:1], scalar2=CLAMP, op0=ALU.add, op1=ALU.min
+                    out=capped[:], in0=live[("o", v)][:], scalar1=bs[:, 0:1], scalar2=CLAMP, op0=ALU.add, op1=ALU.min
                 )
-                live[("capped", k)] = capped
+                live[("capped", v)] = capped
 
-        def clamp_low(k):
-            if is_s(k):
+        def clamp_low(v):
+            if is_s(v):
                 log_s = work.tile([P, COLS], F32, name="log_s", tag="log_s")
-                nc.vector.tensor_scalar_max(out=log_s[:], in0=live[("capped", k)][:], scalar1=-CLAMP)
-                live[("log_s", k)] = log_s
+                nc.vector.tensor_scalar_max(out=log_s[:], in0=live[("capped", v)][:], scalar1=-CLAMP)
+                live[("log_s", v)] = log_s
 
-        def exp(k):
-            if is_s(k):
+        def exp(v):
+            if is_s(v):
                 scale = work.tile([P, COLS], F32, name="scale", tag="scale")
-                nc.scalar.activation(out=scale[:], in_=live[("log_s", k)][:], func=FN.Exp)
-                live[("scale", k)] = scale
+                nc.scalar.activation(out=scale[:], in_=live[("log_s", v)][:], func=FN.Exp)
+                live[("scale", v)] = scale
 
-        def row_sums(k):
-            if is_s(k):
+        def row_sums(v):
+            if is_s(v):
                 bank = small.tile([P, COLS], F32, name="bank", tag="small")
                 for j in range(GROUP):
                     nc.tensor.matmul(
                         out=bank[:, 2 * j : 2 * j + 2],
-                        lhsT=live[("log_s", k)][:, j * P : (j + 1) * P],
+                        lhsT=live[("log_s", v)][:, j * P : (j + 1) * P],
                         rhs=ones_f[:],
                         start=True,
                         stop=True,
                     )
-                live[("sum_bank", k)] = bank
+                live[("sum_bank", v)] = bank
 
-        def row_sums_copy(k):
-            if is_s(k):
-                first = (k // 2) * GROUP
+        def row_sums_copy(v):
+            if is_s(v):
+                first = (v // 2) * GROUP
                 nc.vector.tensor_copy(
                     out=log_det[:, first : first + GROUP],
-                    in_=live[("sum_bank", k)][:, 0 : 2 * GROUP].rearrange("p (j c) -> p j c", c=2)[:, :, 0],
+                    in_=live[("sum_bank", v)][:, 0 : 2 * GROUP].rearrange("p (j c) -> p j c", c=2)[:, :, 0],
                 )
 
-        def exp_back(k):
-            if is_s(k):
+        def exp_back(v):
+            if is_s(v):
                 bank = small.tile([P, COLS], F32, name="bank", tag="small")
                 for j in range(GROUP):
                     nc.tensor.transpose(
-                        bank[:, j * P : (j + 1) * P], live[("scale", k)][:, j * P : (j + 1) * P], ident[:]
+                        bank[:, j * P : (j + 1) * P], live[("scale", v)][:, j * P : (j + 1) * P], ident[:]
                     )
-                live[("scale_bank", k)] = bank
+                live[("scale_bank", v)] = bank
 
-        def times_z2(k):
-            if is_s(k):
+        def times_z2(v):
+            if is_s(v):
                 scaled = work.tile([P, COLS], F32, name="scaled", tag="scaled")
                 nc.vector.tensor_tensor(
-                    out=by_tile(scaled[:]), in0=by_tile(live[("scale_bank", k)][:]), in1=z_half(z_rows[k // 2], 1), op=ALU.mult
+                    out=by_tile(scaled[:]), in0=by_tile(live[("scale_bank", v)][:]), in1=z_part(z_rows[v // 2], 1), op=ALU.mult
                 )
-                live[("scaled", k)] = scaled
+                live[("scaled", v)] = scaled
 
-        def cast_z1(k):
-            if is_s(k):
+        def cast_z1(v):
+            if is_s(v):
                 z_out = work.tile([P, GROUP * 2 * HALF], F32, name="z_out", tag="z_out", bufs=UNITS // 2)
                 nc.gpsimd.tensor_scalar(
-                    out=z_half(z_out, 0), in0=z_half(z_rows[k // 2], 0), scalar1=1.0, scalar2=0.0, op0=ALU.mult, op1=ALU.add
+                    out=z_part(z_out, 0), in0=z_part(z_rows[v // 2], 0), scalar1=1.0, scalar2=0.0, op0=ALU.mult, op1=ALU.add
                 )
-                live[("z_out", k // 2)] = z_out
+                live[("z_out", v // 2)] = z_out
 
-        def shift_bias(k):
-            if is_t(k):
+        def shift_bias(v):
+            if is_t(v):
                 shift = work.tile([P, COLS], F32, name="shift", tag="shift")
                 nc.vector.tensor_tensor(
                     out=by_tile(shift[:]),
-                    in0=by_tile(live[("o", k)][:]),
-                    in1=bias_all[:, HALF : 2 * HALF].unsqueeze(1).to_broadcast([P, GROUP, HALF]),
+                    in0=by_tile(live[("o", v)][:]),
+                    in1=bt_all[:].unsqueeze(1).to_broadcast([P, GROUP, HALF]),
                     op=ALU.add,
                 )
-                live[("shift", k)] = shift
+                live[("shift", v)] = shift
 
-        def add_and_store(k):
-            if is_t(k):
-                g = k // 2
+        def add_and_store(v):
+            if is_t(v):
+                grp = v // 2
                 nc.vector.tensor_tensor(
-                    out=z_half(live[("z_out", g)], 1),
-                    in0=by_tile(live[("shift", k)][:]),
-                    in1=by_tile(live[("scaled", k - 1)][:]),
+                    out=z_part(live[("z_out", grp)], 1),
+                    in0=by_tile(live[("shift", v)][:]),
+                    in1=by_tile(live[("scaled", v - 1)][:]),
                     op=ALU.add,
                 )
                 nc.sync.dma_start(
-                    out=z_out_view[:, g * GROUP : (g + 1) * GROUP, :],
-                    in_=live[("z_out", g)][:].rearrange("p (j d) -> p j d", j=GROUP),
+                    out=z_out_view[:, grp * GROUP : (grp + 1) * GROUP, :],
+                    in_=live[("z_out", grp)][:].rearrange("p (j d) -> p j d", j=GROUP),
                 )
 
         for i in range(-3, UNITS + 4):
             relu_out(i, 0)
             layer1(i, 2)
             wout_copy(i - 1)
-            bias_copy(i - 1)
+            bias_copies(i - 1)
             w1_quantise(i + 1)
             clamp_low(i - 2)
             relu_out(i, 1)

@@ -105,7 +105,9 @@ def tile_affinecouplinglayer_pa_kernel(
         wo_codes = keep.tile([P, 2 * HALF], U32, name="wo_codes", align_bytes=64)
         wo_scales = keep.tile([P, 2 * HALF], U8, name="wo_scales", align_bytes=64)
         bt_all = keep.tile([P, HALF], F32, name="bt_all")
-        bs = keep.tile([P, 1], F32, name="bs")
+        sum_bs = keep.tile([P, 1], F32, name="sum_bs")
+        clamp_lo = keep.tile([P, 1], F32, name="clamp_lo")
+        clamp_hi = keep.tile([P, 1], F32, name="clamp_hi")
         log_det = keep.tile([P, TILES], F32, name="log_det")
         live = {}
 
@@ -145,6 +147,11 @@ def tile_affinecouplinglayer_pa_kernel(
         def z_part(z_tile, part):
             return z_tile[:].rearrange("p (j d) -> p j d", j=GROUP)[:, :, part * HALF : (part + 1) * HALF]
 
+        def store(grp, part, half):
+            nc.sync.dma_start(
+                out=z_out_view[:, grp * GROUP : (grp + 1) * GROUP, part * HALF : (part + 1) * HALF], in_=by_tile(half[:])
+            )
+
         def w1_transposes(v):
             if v in (0, 1):
                 live[("w1_bank", v)] = [transpose_words(w1_rows[v], first) for first in PAIRS]
@@ -180,12 +187,17 @@ def tile_affinecouplinglayer_pa_kernel(
             if v == 0:
                 bank = small.tile([P, COLS], F32, name="bank", tag="small")
                 nc.tensor.matmul(out=bank[:, 0:HALF], lhsT=ones_bf[:], rhs=bt_rows[:], start=True, stop=True)
+                nc.tensor.matmul(out=bank[:, HALF : HALF + 1], lhsT=ones_bf[:], rhs=bs_bf[:], start=True, stop=True)
                 live["bt_bank"] = bank
 
         def bias_copies(v):
             if v == 0:
                 nc.vector.tensor_copy(out=bt_all[:], in_=live["bt_bank"][:, 0:HALF])
-                nc.vector.tensor_copy(out=bs[:], in_=bs_bf[:])
+                nc.vector.tensor_copy(out=sum_bs[:], in_=live["bt_bank"][:, HALF : HALF + 1])
+                for bound, value in ((clamp_lo, -CLAMP), (clamp_hi, CLAMP)):
+                    nc.vector.tensor_scalar(
+                        out=bound[:], in0=bs_bf[:], scalar1=-1.0, scalar2=value, op0=ALU.mult, op1=ALU.add
+                    )
 
         def h_transposes(v):
             if is_unit(v):
@@ -276,24 +288,23 @@ def tile_affinecouplinglayer_pa_kernel(
                     )
                 live[("o", v)] = product
 
-        def bias_clamp_high(v):
+        def clamp(v):
             if is_s(v):
-                capped = work.tile([P, COLS], F32, name="capped", tag="capped")
+                unbiased = work.tile([P, COLS], F32, name="unbiased", tag="unbiased")
                 nc.vector.tensor_scalar(
-                    out=capped[:], in0=live[("o", v)][:], scalar1=bs[:, 0:1], scalar2=CLAMP, op0=ALU.add, op1=ALU.min
+                    out=unbiased[:],
+                    in0=live[("o", v)][:],
+                    scalar1=clamp_lo[:, 0:1],
+                    scalar2=clamp_hi[:, 0:1],
+                    op0=ALU.max,
+                    op1=ALU.min,
                 )
-                live[("capped", v)] = capped
-
-        def clamp_low(v):
-            if is_s(v):
-                log_s = work.tile([P, COLS], F32, name="log_s", tag="log_s")
-                nc.vector.tensor_scalar_max(out=log_s[:], in0=live[("capped", v)][:], scalar1=-CLAMP)
-                live[("log_s", v)] = log_s
+                live[("unbiased", v)] = unbiased
 
         def exp(v):
             if is_s(v):
                 scale = work.tile([P, COLS], F32, name="scale", tag="scale")
-                nc.scalar.activation(out=scale[:], in_=live[("log_s", v)][:], func=FN.Exp)
+                nc.scalar.activation(out=scale[:], in_=live[("unbiased", v)][:], func=FN.Exp, bias=bs_bf[:, 0:1])
                 live[("scale", v)] = scale
 
         def row_sums(v):
@@ -302,7 +313,7 @@ def tile_affinecouplinglayer_pa_kernel(
                 for j in range(GROUP):
                     nc.tensor.matmul(
                         out=bank[:, 2 * j : 2 * j + 2],
-                        lhsT=live[("log_s", v)][:, j * P : (j + 1) * P],
+                        lhsT=live[("unbiased", v)][:, j * P : (j + 1) * P],
                         rhs=ones_f[:],
                         start=True,
                         stop=True,
@@ -312,9 +323,13 @@ def tile_affinecouplinglayer_pa_kernel(
         def row_sums_copy(v):
             if is_s(v):
                 first = (v // 2) * GROUP
-                nc.vector.tensor_copy(
+                nc.vector.tensor_scalar(
                     out=log_det[:, first : first + GROUP],
-                    in_=live[("sum_bank", v)][:, 0 : 2 * GROUP].rearrange("p (j c) -> p j c", c=2)[:, :, 0],
+                    in0=live[("sum_bank", v)][:, 0 : 2 * GROUP].rearrange("p (j c) -> p j c", c=2)[:, :, 0],
+                    scalar1=sum_bs[:, 0:1],
+                    scalar2=0.0,
+                    op0=ALU.add,
+                    op1=ALU.add,
                 )
 
         def exp_back(v):
@@ -334,13 +349,11 @@ def tile_affinecouplinglayer_pa_kernel(
                 )
                 live[("scaled", v)] = scaled
 
-        def cast_z1(v):
-            if is_s(v):
-                z_out = work.tile([P, GROUP * 2 * HALF], F32, name="z_out", tag="z_out", bufs=UNITS // 2)
-                nc.gpsimd.tensor_scalar(
-                    out=z_part(z_out, 0), in0=z_part(z_rows[v // 2], 0), scalar1=1.0, scalar2=0.0, op0=ALU.mult, op1=ALU.add
-                )
-                live[("z_out", v // 2)] = z_out
+        def cast_z1(grp):
+            if 0 <= grp < UNITS // 2:
+                z1_out = keep.tile([P, COLS], F32, name="z1_out%d" % grp)
+                nc.scalar.copy(out=by_tile(z1_out[:]), in_=z_part(z_rows[grp], 0))
+                store(grp, 0, z1_out)
 
         def shift_bias(v):
             if is_t(v):
@@ -355,17 +368,11 @@ def tile_affinecouplinglayer_pa_kernel(
 
         def add_and_store(v):
             if is_t(v):
-                grp = v // 2
+                z2_out = keep.tile([P, COLS], F32, name="z2_out%d" % (v // 2))
                 nc.vector.tensor_tensor(
-                    out=z_part(live[("z_out", grp)], 1),
-                    in0=by_tile(live[("shift", v)][:]),
-                    in1=by_tile(live[("scaled", v - 1)][:]),
-                    op=ALU.add,
+                    out=z2_out[:], in0=live[("shift", v)][:], in1=live[("scaled", v - 1)][:], op=ALU.add
                 )
-                nc.sync.dma_start(
-                    out=z_out_view[:, grp * GROUP : (grp + 1) * GROUP, :],
-                    in_=live[("z_out", grp)][:].rearrange("p (j d) -> p j d", j=GROUP),
-                )
+                store(v // 2, 1, z2_out)
 
         for i in range(-3, UNITS + 4):
             relu_out(i, 0)
@@ -373,7 +380,6 @@ def tile_affinecouplinglayer_pa_kernel(
             wout_copy(i - 1)
             bias_copies(i - 1)
             w1_quantise(i + 1)
-            clamp_low(i - 2)
             relu_out(i, 1)
             layer1(i, 3)
             exp_back(i - 4)
@@ -389,13 +395,13 @@ def tile_affinecouplinglayer_pa_kernel(
             layer1(i + 1, 0)
             times_z2(i - 4)
             shift_bias(i - 2)
-            cast_z1(i)
             wout_transposes(i)
-            bias_clamp_high(i - 1)
+            clamp(i - 1)
             relu_out(i, 3)
             layer1(i + 1, 1)
             w1_copies(i + 2)
             exp(i - 2)
+            cast_z1(i - (UNITS - 2))
             h_copies(i + 2)
             regroup(i)
             row_sums_copy(i - 3)

@@ -19,11 +19,14 @@ HALF = 128
 TILES = ROWS // P
 GROUP = 4
 COLS = GROUP * P
-UNITS = 2 * TILES // GROUP
+GROUPS = TILES // GROUP
 WORDS = HID // 2
-PAIRS = (0, 2)
+PAIR = 2
 CLAMP = 2.0
 FLOPS = 2 * 2 * ROWS * HID * (HID + HALF)
+PARTS = [(n, g * GROUP, GROUP) for g in range(GROUPS) for n in range(2)]
+PARTS[-1:] = [(1, 12, 4)]
+UNITS = len(PARTS)
 
 
 def tile_affinecouplinglayer_pa_kernel(
@@ -48,7 +51,6 @@ def tile_affinecouplinglayer_pa_kernel(
         warm_in = keep.tile([P, 1], F32, name="warm_in")
         warm_out = keep.tile([P, 1], F32, name="warm_out")
         nc.vector.memset(warm_in[:], 0.0)
-        nc.scalar.activation(out=warm_out[:], in_=warm_in[:], func=FN.Exp)
         ones_bf = keep.tile([P, P], BF16, name="ones_bf")
         nc.vector.memset(ones_bf[:], 1.0)
         ones_f = keep.tile([P, 2], F32, name="ones_f")
@@ -57,55 +59,61 @@ def tile_affinecouplinglayer_pa_kernel(
         nc.vector.memset(bt_rows[:], 0.0)
 
         h_view = [h_in[n].rearrange("(p i) k -> p i k", i=TILES) for n in range(2)]
+        w1_view = [w1_in[n].rearrange("(m t) k -> m t k", t=PACK) for n in range(2)]
         z_view = z.rearrange("(p i) d -> p i d", i=TILES)
         z_out_view = out_0.rearrange("(p i) d -> p i d", i=TILES)
 
-        w1_rows = [keep.tile([P, PACK * HID], BF16, name="w1_rows%d" % n) for n in range(2)]
-        b1_bf = [keep.tile([P, PACK], BF16, name="b1_bf%d" % n) for n in range(2)]
+        w1_rows = [[keep.tile([P, PAIR * HID], BF16, name="w1_rows%d_%d" % (n, q)) for q in range(2)] for n in range(2)]
+        h_rows = [[keep.tile([P, PAIR * HID], BF16, name="h_rows%d_%d" % (n, q)) for q in range(TILES // PAIR)] for n in range(2)]
+        b1 = [keep.tile([P, PACK], BF16, name="b1_%d" % n) for n in range(2)]
         wo_rows = [keep.tile([P, HID], BF16, name="wo_rows%d" % n) for n in range(2)]
-        bs_bf = keep.tile([P, 1], BF16, name="bs_bf")
-        h_rows = [keep.tile([P, GROUP * HID], BF16, name="h_rows%d" % v) for v in range(UNITS)]
-        z_rows = [keep.tile([P, GROUP * 2 * HALF], BF16, name="z_rows%d" % grp) for grp in range(UNITS // 2)]
+        bs = keep.tile([P, 1], BF16, name="bs")
+        z_rows = [keep.tile([P, GROUP * 2 * HALF], BF16, name="z_rows%d" % g) for g in range(GROUPS)]
 
-        def load_h(v):
-            first = (v // 2) * GROUP
+        def load_w1(n):
+            for q in range(2):
+                nc.sync.dma_start(
+                    out=w1_rows[n][q][:].rearrange("m (t k) -> m t k", t=PAIR),
+                    in_=w1_view[n][:, PAIR * q : PAIR * (q + 1), :],
+                )
+
+        def load_h(g, n):
+            for q in range(2 * g, 2 * g + 2):
+                nc.sync.dma_start(
+                    out=h_rows[n][q][:].rearrange("p (j k) -> p j k", j=PAIR),
+                    in_=h_view[n][:, PAIR * q : PAIR * (q + 1), :],
+                )
+
+        def load_z(g):
             nc.sync.dma_start(
-                out=h_rows[v][:].rearrange("p (j k) -> p j k", j=GROUP),
-                in_=h_view[v % 2][:, first : first + GROUP, :],
+                out=z_rows[g][:].rearrange("p (j d) -> p j d", j=GROUP),
+                in_=z_view[:, g * GROUP : (g + 1) * GROUP, :],
             )
 
-        def load_z(grp):
-            nc.sync.dma_start(
-                out=z_rows[grp][:].rearrange("p (j d) -> p j d", j=GROUP),
-                in_=z_view[:, grp * GROUP : (grp + 1) * GROUP, :],
-            )
-
+        nc.scalar.dma_start(out=bt_rows[0:1, :], in_=t_bout.rearrange("(o c) -> o c", o=1))
+        nc.scalar.dma_start(out=bs[:], in_=s_bout.rearrange("(o c) -> o c", c=1))
         for n in range(2):
-            nc.sync.dma_start(
-                out=w1_rows[n][:].rearrange("m (t k) -> m t k", t=PACK),
-                in_=w1_in[n].rearrange("(m t) k -> m t k", t=PACK),
-            )
-            load_h(n)
-            nc.sync.dma_start(out=b1_bf[n][:], in_=b1_in[n].rearrange("(m t) -> m t", t=PACK))
+            nc.scalar.dma_start(out=b1[n][:], in_=b1_in[n].rearrange("(m t) -> m t", t=PACK))
+        nc.scalar.activation(out=warm_out[:], in_=warm_in[:], func=FN.Exp)
+        load_w1(0)
+        load_h(0, 0)
         for n in range(2):
             nc.sync.dma_start(out=wo_rows[n][:], in_=wo_in[n])
-        nc.sync.dma_start(out=bt_rows[0:1, :], in_=t_bout.rearrange("(o c) -> o c", o=1))
-        nc.sync.dma_start(out=bs_bf[:], in_=s_bout.rearrange("(o c) -> o c", c=1))
-        for grp in range(1, UNITS // 2):
-            load_h(2 * grp)
-            load_h(2 * grp + 1)
-            load_z(grp - 1)
-        load_z(UNITS // 2 - 1)
+        load_w1(1)
+        load_h(0, 1)
+        for g in range(1, GROUPS):
+            load_h(g, 0)
+            load_h(g, 1)
+            load_z(g - 1)
+        load_z(GROUPS - 1)
 
         w1_grouped = [keep.tile([P, PACK * HID], BF16, name="w1_grouped%d" % n, align_bytes=64) for n in range(2)]
         w1_codes = [keep.tile([P, HID], U32, name="w1_codes%d" % n, align_bytes=64) for n in range(2)]
         w1_scales = [keep.tile([P, HID], U8, name="w1_scales%d" % n, align_bytes=64) for n in range(2)]
-        b1 = [keep.tile([P, PACK], F32, name="b1_%d" % n) for n in range(2)]
         wo_grouped = keep.tile([P, 2 * HALF * PACK], BF16, name="wo_grouped", align_bytes=64)
         wo_codes = keep.tile([P, 2 * HALF], U32, name="wo_codes", align_bytes=64)
         wo_scales = keep.tile([P, 2 * HALF], U8, name="wo_scales", align_bytes=64)
-        bt_all = keep.tile([P, HALF], F32, name="bt_all")
-        sum_bs = keep.tile([P, 1], F32, name="sum_bs")
+        bias_row = keep.tile([P, HALF + 1], F32, name="bias_row")
         clamp_lo = keep.tile([P, 1], F32, name="clamp_lo")
         clamp_hi = keep.tile([P, 1], F32, name="clamp_hi")
         log_det = keep.tile([P, TILES], F32, name="log_det")
@@ -115,19 +123,25 @@ def tile_affinecouplinglayer_pa_kernel(
             return 0 <= v < UNITS
 
         def is_s(v):
-            return is_unit(v) and v % 2 == 0
+            return is_unit(v) and PARTS[v][0] == 0
 
         def is_t(v):
-            return is_unit(v) and v % 2 == 1
+            return is_unit(v) and PARTS[v][0] == 1
 
-        def transpose_words(rows, first):
+        def width(v):
+            return PARTS[v][2] * P
+
+        def group(v):
+            return PARTS[v][1] // GROUP
+
+        def transpose_words(rows):
             words = rows[:].bitcast(F32)
             bank = small.tile([P, COLS], F32, name="bank", tag="small")
             for j in range(2):
                 for u in range(2):
                     nc.tensor.transpose(
                         bank[:, (2 * u + j) * P : (2 * u + j + 1) * P],
-                        words[:, (first + j) * WORDS + u * P : (first + j) * WORDS + (u + 1) * P],
+                        words[:, j * WORDS + u * P : j * WORDS + (u + 1) * P],
                         ident[:],
                     )
             return bank
@@ -142,85 +156,72 @@ def tile_affinecouplinglayer_pa_kernel(
             nc.vector.quantize_mx(out=codes[:].bitcast(FP8X4), scales=scales[:], in_=grouped[:])
 
         def by_tile(ap):
-            return ap.rearrange("p (j c) -> p j c", j=GROUP)
+            return ap.rearrange("p (j c) -> p j c", c=P)
 
         def z_part(z_tile, part):
-            return z_tile[:].rearrange("p (j d) -> p j d", j=GROUP)[:, :, part * HALF : (part + 1) * HALF]
+            return z_tile[:].rearrange("p (j d) -> p j d", d=2 * HALF)[:, :, part * HALF : (part + 1) * HALF]
 
-        def store(grp, part, half):
+        def store(first, count, part, half):
             nc.sync.dma_start(
-                out=z_out_view[:, grp * GROUP : (grp + 1) * GROUP, part * HALF : (part + 1) * HALF], in_=by_tile(half[:])
+                out=z_out_view[:, first : first + count, part * HALF : (part + 1) * HALF], in_=by_tile(half)
             )
 
-        def w1_transposes(v):
-            if v in (0, 1):
-                live[("w1_bank", v)] = [transpose_words(w1_rows[v], first) for first in PAIRS]
+        def w1_transposes(n):
+            live[("w1_bank", n)] = [transpose_words(w1_rows[n][q]) for q in range(2)]
 
-        def w1_copies(v):
-            if v in (0, 1):
-                interleave(nc.scalar.copy, live[("w1_bank", v)][0], w1_grouped[v], PAIRS[0])
-                interleave(nc.vector.tensor_copy, live[("w1_bank", v)][1], w1_grouped[v], PAIRS[1])
+        def w1_copies(n, copies):
+            for q in range(2):
+                interleave(copies[q], live[("w1_bank", n)][q], w1_grouped[n], PAIR * q)
 
-        def w1_quantise(v):
-            if v in (0, 1):
-                quantise(w1_grouped[v], w1_codes[v], w1_scales[v])
-                nc.vector.tensor_copy(out=b1[v][:], in_=b1_bf[v][:])
+        def w1_quantise(n):
+            quantise(w1_grouped[n], w1_codes[n], w1_scales[n])
 
-        def wout_transposes(v):
-            if v == 0:
-                bank = small.tile([P, COLS], F32, name="bank", tag="small")
-                for n in range(2):
-                    words = wo_rows[n][:].bitcast(F32).rearrange("c (p u) -> c p u", u=2)
-                    for u in range(2):
-                        nc.tensor.transpose(bank[:, (2 * u + n) * P : (2 * u + n + 1) * P], words[:, :, u], ident[:])
-                live["wo_bank"] = bank
+        def wout_transposes():
+            bank = small.tile([P, COLS], F32, name="bank", tag="small")
+            for n in range(2):
+                words = wo_rows[n][:].bitcast(F32).rearrange("c (p u) -> c p u", u=2)
+                for u in range(2):
+                    nc.tensor.transpose(bank[:, (2 * u + n) * P : (2 * u + n + 1) * P], words[:, :, u], ident[:])
+            live["wo_bank"] = bank
 
-        def wout_copy(v):
-            if v == 0:
-                interleave(nc.vector.tensor_copy, live["wo_bank"], wo_grouped, 0)
+        def wout_copy(copy):
+            interleave(copy, live["wo_bank"], wo_grouped, 0)
 
-        def wout_quantise(v):
-            if v == 0:
-                quantise(wo_grouped, wo_codes, wo_scales)
+        def wout_quantise():
+            quantise(wo_grouped, wo_codes, wo_scales)
 
-        def bias_matmul(v):
-            if v == 0:
-                bank = small.tile([P, COLS], F32, name="bank", tag="small")
-                nc.tensor.matmul(out=bank[:, 0:HALF], lhsT=ones_bf[:], rhs=bt_rows[:], start=True, stop=True)
-                nc.tensor.matmul(out=bank[:, HALF : HALF + 1], lhsT=ones_bf[:], rhs=bs_bf[:], start=True, stop=True)
-                live["bt_bank"] = bank
-
-        def bias_copies(v):
-            if v == 0:
-                nc.vector.tensor_copy(out=bt_all[:], in_=live["bt_bank"][:, 0:HALF])
-                nc.vector.tensor_copy(out=sum_bs[:], in_=live["bt_bank"][:, HALF : HALF + 1])
-                for bound, value in ((clamp_lo, -CLAMP), (clamp_hi, CLAMP)):
-                    nc.vector.tensor_scalar(
-                        out=bound[:], in0=bs_bf[:], scalar1=-1.0, scalar2=value, op0=ALU.mult, op1=ALU.add
-                    )
+        def bias_matmuls():
+            bank = small.tile([P, COLS], F32, name="bank", tag="small")
+            nc.tensor.matmul(out=bank[:, 0:HALF], lhsT=ones_bf[:], rhs=bt_rows[:], start=True, stop=True)
+            nc.tensor.matmul(out=bank[:, HALF : HALF + 1], lhsT=ones_bf[:], rhs=bs[:], start=True, stop=True)
+            nc.vector.tensor_copy(out=bias_row[:], in_=bank[:, 0 : HALF + 1])
+            for bound, value in ((clamp_lo, -CLAMP), (clamp_hi, CLAMP)):
+                nc.vector.tensor_scalar(out=bound[:], in0=bs[:], scalar1=-1.0, scalar2=value, op0=ALU.mult, op1=ALU.add)
 
         def h_transposes(v):
             if is_unit(v):
-                live[("h_grouped", v)] = work.tile([P, COLS * PACK], BF16, name="h_grouped", tag="h_grouped", align_bytes=64)
-                live[("h_bank", v)] = [transpose_words(h_rows[v], first) for first in PAIRS]
+                n, first, count = PARTS[v]
+                live[("h_grouped", v)] = work.tile([P, width(v) * PACK], BF16, name="h_grouped", tag="h_grouped", align_bytes=64)
+                live[("h_bank", v)] = [transpose_words(h_rows[n][first // PAIR + q]) for q in range(count // PAIR)]
 
         def h_copies(v):
             if is_unit(v):
-                for pair in range(2):
-                    interleave(nc.scalar.copy, live[("h_bank", v)][pair], live[("h_grouped", v)], PAIRS[pair])
+                for pair, bank in enumerate(live[("h_bank", v)]):
+                    copy = nc.vector.tensor_copy if v in (1, 3) else nc.scalar.copy
+                    interleave(copy, bank, live[("h_grouped", v)], PAIR * pair)
 
         def h_quantise(v):
             if is_unit(v):
-                codes = work.tile([P, COLS], U32, name="h_codes", tag="h_codes", bufs=3, align_bytes=64)
-                scales = work.tile([P, COLS], U8, name="h_scales", tag="h_scales", bufs=3, align_bytes=64)
+                codes = work.tile([P, width(v)], U32, name="h_codes", tag="h_codes", bufs=3, align_bytes=64)
+                scales = work.tile([P, width(v)], U8, name="h_scales", tag="h_scales", bufs=3, align_bytes=64)
                 quantise(live[("h_grouped", v)], codes, scales)
                 live[("h_codes", v)] = (codes, scales)
 
         def layer1(v, t):
             if is_unit(v):
-                n = v % 2
+                n = PARTS[v][0]
                 codes, scales = live[("h_codes", v)]
-                acc = acc1.tile([P, COLS], F32, name="acc", tag="acc1")
+                acc = acc1.tile([P, width(v)], F32, name="acc", tag="acc1")
                 nc.tensor.matmul_mx(
                     out=acc[:],
                     lhsT=w1_codes[n][:, t * P : (t + 1) * P].bitcast(FP8X4),
@@ -235,17 +236,17 @@ def tile_affinecouplinglayer_pa_kernel(
         def relu_out(v, t):
             if is_unit(v):
                 if t == 0:
-                    live[("g", v)] = work.tile([P, PACK * COLS], BF16, name="g", tag="g")
+                    live[("g", v)] = work.tile([P, PACK * width(v)], BF16, name="g", tag="g")
                 nc.scalar.activation(
-                    out=live[("g", v)][:, t * COLS : (t + 1) * COLS],
+                    out=live[("g", v)][:, t * width(v) : (t + 1) * width(v)],
                     in_=live[("acc", v, t)][:],
                     func=FN.Relu,
-                    bias=b1[v % 2][:, t : t + 1],
+                    bias=b1[PARTS[v][0]][:, t : t + 1],
                 )
 
         def regroup(v):
             if is_unit(v):
-                grouped = work.tile([P, COLS * PACK], BF16, name="g_grouped", tag="g_grouped", align_bytes=64)
+                grouped = work.tile([P, width(v) * PACK], BF16, name="g_grouped", tag="g_grouped", align_bytes=64)
                 nc.vector.tensor_copy(
                     out=grouped[:].rearrange("p (c r t) -> p c t r", r=4, t=PACK),
                     in_=live[("g", v)][:].rearrange("p (t c r) -> p c t r", t=PACK, r=4),
@@ -254,8 +255,8 @@ def tile_affinecouplinglayer_pa_kernel(
 
         def g_quantise(v):
             if is_unit(v):
-                codes = work.tile([P, COLS], U32, name="g_codes", tag="g_codes", align_bytes=64)
-                scales = work.tile([P, COLS], U8, name="g_scales", tag="g_scales", align_bytes=64)
+                codes = work.tile([P, width(v)], U32, name="g_codes", tag="g_codes", align_bytes=64)
+                scales = work.tile([P, width(v)], U8, name="g_scales", tag="g_scales", align_bytes=64)
                 quantise(live[("g_grouped", v)], codes, scales)
                 live[("g_codes", v)] = (codes, scales)
 
@@ -275,8 +276,11 @@ def tile_affinecouplinglayer_pa_kernel(
                 live[("o", v)] = product
             if is_t(v):
                 codes, scales = live[("g_codes", v)]
-                product = acc2.tile([P, COLS], F32, name="o_t", tag="o_t")
-                for j in range(GROUP):
+                if v == UNITS - 1 and width(v) < COLS:
+                    product = acc1.tile([P, width(v)], F32, name="acc", tag="acc1")
+                else:
+                    product = acc2.tile([P, width(v)], F32, name="o_t", tag="o_t")
+                for j in range(PARTS[v][2]):
                     nc.tensor.matmul_mx(
                         out=product[:, j * P : (j + 1) * P],
                         lhsT=codes[:, j * P : (j + 1) * P].bitcast(FP8X4),
@@ -304,29 +308,27 @@ def tile_affinecouplinglayer_pa_kernel(
         def exp(v):
             if is_s(v):
                 scale = work.tile([P, COLS], F32, name="scale", tag="scale")
-                nc.scalar.activation(out=scale[:], in_=live[("unbiased", v)][:], func=FN.Exp, bias=bs_bf[:, 0:1])
+                nc.scalar.activation(out=scale[:], in_=live[("unbiased", v)][:], func=FN.Exp, bias=bs[:, 0:1])
                 live[("scale", v)] = scale
 
         def row_sums(v):
             if is_s(v):
-                bank = small.tile([P, COLS], F32, name="bank", tag="small")
                 for j in range(GROUP):
                     nc.tensor.matmul(
-                        out=bank[:, 2 * j : 2 * j + 2],
+                        out=live[("o", v)][:, 2 * j : 2 * j + 2],
                         lhsT=live[("unbiased", v)][:, j * P : (j + 1) * P],
                         rhs=ones_f[:],
                         start=True,
                         stop=True,
                     )
-                live[("sum_bank", v)] = bank
 
         def row_sums_copy(v):
             if is_s(v):
-                first = (v // 2) * GROUP
+                first = PARTS[v][1]
                 nc.vector.tensor_scalar(
                     out=log_det[:, first : first + GROUP],
-                    in0=live[("sum_bank", v)][:, 0 : 2 * GROUP].rearrange("p (j c) -> p j c", c=2)[:, :, 0],
-                    scalar1=sum_bs[:, 0:1],
+                    in0=live[("o", v)][:, 0 : 2 * GROUP].rearrange("p (j c) -> p j c", c=2)[:, :, 0],
+                    scalar1=bias_row[:, HALF : HALF + 1],
                     scalar2=0.0,
                     op0=ALU.add,
                     op1=ALU.add,
@@ -345,65 +347,77 @@ def tile_affinecouplinglayer_pa_kernel(
             if is_s(v):
                 scaled = work.tile([P, COLS], F32, name="scaled", tag="scaled")
                 nc.vector.tensor_tensor(
-                    out=by_tile(scaled[:]), in0=by_tile(live[("scale_bank", v)][:]), in1=z_part(z_rows[v // 2], 1), op=ALU.mult
+                    out=by_tile(scaled[:]), in0=by_tile(live[("scale_bank", v)][:]), in1=z_part(z_rows[group(v)], 1), op=ALU.mult
                 )
                 live[("scaled", v)] = scaled
 
-        def cast_z1(grp):
-            if 0 <= grp < UNITS // 2:
-                z1_out = keep.tile([P, COLS], F32, name="z1_out%d" % grp)
-                nc.scalar.copy(out=by_tile(z1_out[:]), in_=z_part(z_rows[grp], 0))
-                store(grp, 0, z1_out)
-
-        def shift_bias(v):
-            if is_t(v):
-                shift = work.tile([P, COLS], F32, name="shift", tag="shift")
+        def add_bias(v):
+            if is_s(v):
+                biased = work.tile([P, COLS], F32, name="biased", tag="biased")
                 nc.vector.tensor_tensor(
-                    out=by_tile(shift[:]),
-                    in0=by_tile(live[("o", v)][:]),
-                    in1=bt_all[:].unsqueeze(1).to_broadcast([P, GROUP, HALF]),
+                    out=by_tile(biased[:]),
+                    in0=by_tile(live[("scaled", v)][:]),
+                    in1=bias_row[:, 0:HALF].unsqueeze(1).to_broadcast([P, GROUP, HALF]),
                     op=ALU.add,
                 )
-                live[("shift", v)] = shift
+                live[("biased", group(v))] = biased
 
         def add_and_store(v):
             if is_t(v):
-                z2_out = keep.tile([P, COLS], F32, name="z2_out%d" % (v // 2))
+                n, first, count = PARTS[v]
+                z2_out = keep.tile([P, width(v)], F32, name="z2_out%d" % v)
+                at = (first % GROUP) * P
                 nc.vector.tensor_tensor(
-                    out=z2_out[:], in0=live[("shift", v)][:], in1=live[("scaled", v - 1)][:], op=ALU.add
+                    out=z2_out[:], in0=live[("o", v)][:], in1=live[("biased", group(v))][:, at : at + width(v)], op=ALU.add
                 )
-                store(v // 2, 1, z2_out)
+                store(first, count, 1, z2_out[:])
 
-        for i in range(-3, UNITS + 4):
+        def cast_z1(g):
+            if 0 <= g < GROUPS:
+                z1_out = keep.tile([P, COLS], F32, name="z1_out%d" % g)
+                nc.scalar.copy(out=by_tile(z1_out[:]), in_=z_part(z_rows[g], 0))
+                store(g * GROUP, GROUP, 0, z1_out[:])
+
+        A, V = nc.scalar.copy, nc.vector.tensor_copy
+        w1_transposes(0)
+        w1_copies(0, (A, V))
+        h_transposes(0)
+        w1_quantise(0)
+        h_copies(0)
+        wout_transposes()
+        h_quantise(0)
+        w1_transposes(1)
+        wout_copy(V)
+        wout_quantise()
+        layer1(0, 0)
+        layer1(0, 1)
+        w1_copies(1, (A, A))
+        h_transposes(1)
+        w1_quantise(1)
+        h_copies(1)
+        bias_matmuls()
+        for i in range(UNITS + 4):
             relu_out(i, 0)
             layer1(i, 2)
-            wout_copy(i - 1)
-            bias_copies(i - 1)
-            w1_quantise(i + 1)
+            exp(i - 2)
+            add_bias(i - 4)
             relu_out(i, 1)
             layer1(i, 3)
-            exp_back(i - 4)
-            h_transposes(i + 2)
-            add_and_store(i - 4)
             g_quantise(i - 1)
-            wout_quantise(i - 1)
-            w1_transposes(i + 3)
+            h_transposes(i + 2)
+            row_sums(i - 2)
+            exp_back(i - 2)
+            add_and_store(i - 3)
             layer2(i - 1)
             h_quantise(i + 1)
-            row_sums(i - 3)
             relu_out(i, 2)
             layer1(i + 1, 0)
-            times_z2(i - 4)
-            shift_bias(i - 2)
-            wout_transposes(i)
+            times_z2(i - 3)
             clamp(i - 1)
             relu_out(i, 3)
             layer1(i + 1, 1)
-            w1_copies(i + 2)
-            exp(i - 2)
-            cast_z1(i - (UNITS - 2))
             h_copies(i + 2)
             regroup(i)
-            row_sums_copy(i - 3)
-            bias_matmul(i)
+            row_sums_copy(i - 2)
+            cast_z1(i - (UNITS - 2))
         nc.sync.dma_start(out=out_1.rearrange("(p i) -> p i", i=TILES), in_=log_det[:])

@@ -398,26 +398,26 @@ def tile_affinecouplinglayer_pa_kernel(
         bias_matmuls()
         for i in range(UNITS + 4):
             relu_out(i, 0)
+            times_z2(i - 3)
             layer1(i, 2)
-            exp(i - 2)
-            add_bias(i - 4)
             relu_out(i, 1)
             layer1(i, 3)
+            add_and_store(i - 3)
+            h_quantise(i + 1)
             g_quantise(i - 1)
             h_transposes(i + 2)
             row_sums(i - 2)
-            exp_back(i - 2)
-            add_and_store(i - 3)
-            layer2(i - 1)
-            h_quantise(i + 1)
             relu_out(i, 2)
-            layer1(i + 1, 0)
-            times_z2(i - 3)
-            clamp(i - 1)
             relu_out(i, 3)
-            layer1(i + 1, 1)
+            exp(i - 2)
             h_copies(i + 2)
-            regroup(i)
+            layer1(i + 1, 0)
+            layer1(i + 1, 1)
+            exp_back(i - 2)
+            layer2(i - 1)
+            add_bias(i - 3)
+            clamp(i - 1)
             row_sums_copy(i - 2)
+            regroup(i)
             cast_z1(i - (UNITS - 2))
         nc.sync.dma_start(out=out_1.rearrange("(p i) -> p i", i=TILES), in_=log_det[:])

@@ -23,6 +23,8 @@ GROUPS = TILES // GROUP
 WORDS = HID // 2
 PAIR = 2
 CLAMP = 2.0
+PICK = P // TILES
+LAST_S = 2 * (GROUPS - 1)
 FLOPS = 2 * 2 * ROWS * HID * (HID + HALF)
 PARTS = [(n, g * GROUP, GROUP) for g in range(GROUPS) for n in range(2)]
 PARTS[-1:] = [(1, 12, 4)]
@@ -53,8 +55,9 @@ def tile_affinecouplinglayer_pa_kernel(
         nc.vector.memset(warm_in[:], 0.0)
         ones_bf = keep.tile([P, P], BF16, name="ones_bf")
         nc.vector.memset(ones_bf[:], 1.0)
-        ones_f = keep.tile([P, 2], F32, name="ones_f")
-        nc.vector.memset(ones_f[:], 1.0)
+        picks = keep.tile([P, 2 * P - PICK], F32, name="picks")
+        nc.vector.memset(picks[:], 0.0)
+        nc.vector.memset(picks[:, P - PICK : P], 1.0)
         bt_rows = keep.tile([P, HALF], BF16, name="bt_rows")
         nc.vector.memset(bt_rows[:], 0.0)
 
@@ -314,25 +317,41 @@ def tile_affinecouplinglayer_pa_kernel(
         def row_sums(v):
             if is_s(v):
                 for j in range(GROUP):
+                    at = P - PICK - (PARTS[v][1] + j) * PICK
                     nc.tensor.matmul(
-                        out=live[("o", v)][:, 2 * j : 2 * j + 2],
-                        lhsT=live[("unbiased", v)][:, j * P : (j + 1) * P],
-                        rhs=ones_f[:],
-                        start=True,
-                        stop=True,
+                        out=live[("o", v)][:, 0:P],
+                        lhsT=picks[:, at : at + P],
+                        rhs=live[("unbiased", v)][:, j * P : (j + 1) * P],
+                        start=j == 0,
+                        stop=j == GROUP - 1,
                     )
 
-        def row_sums_copy(v):
+        def row_sums_exit(v):
             if is_s(v):
-                first = PARTS[v][1]
+                sums = work.tile([P, P], F32, name="sums", tag="sums")
+                if "sums" in live:
+                    nc.vector.tensor_tensor(out=sums[:], in0=live[("o", v)][:, 0:P], in1=live["sums"][:], op=ALU.add)
+                else:
+                    nc.vector.tensor_copy(out=sums[:], in_=live[("o", v)][:, 0:P])
+                live["sums"] = sums
+
+        def row_sums_turn(v):
+            if v == LAST_S:
+                bank = small.tile([P, COLS], F32, name="bank", tag="small")
+                nc.tensor.transpose(bank[:, 0:P], live["sums"][:], ident[:])
+                live["turned"] = bank
+
+        def row_sums_store(v):
+            if v == LAST_S:
                 nc.vector.tensor_scalar(
-                    out=log_det[:, first : first + GROUP],
-                    in0=live[("o", v)][:, 0 : 2 * GROUP].rearrange("p (j c) -> p j c", c=2)[:, :, 0],
+                    out=log_det[:],
+                    in0=live["turned"][:, 0:P].rearrange("p (i c) -> p i c", c=PICK)[:, :, 0],
                     scalar1=bias_row[:, HALF : HALF + 1],
                     scalar2=0.0,
                     op0=ALU.add,
                     op1=ALU.add,
                 )
+                nc.sync.dma_start(out=out_1.rearrange("(p i) -> p i", i=TILES), in_=log_det[:])
 
         def exp_back(v):
             if is_s(v):
@@ -414,10 +433,11 @@ def tile_affinecouplinglayer_pa_kernel(
             layer1(i + 1, 0)
             layer1(i + 1, 1)
             exp_back(i - 2)
+            row_sums_turn(i - 3)
             layer2(i - 1)
+            row_sums_store(i - 3)
             add_bias(i - 3)
             clamp(i - 1)
-            row_sums_copy(i - 2)
+            row_sums_exit(i - 2)
             regroup(i)
             cast_z1(i - (UNITS - 2))
-        nc.sync.dma_start(out=out_1.rearrange("(p i) -> p i", i=TILES), in_=log_det[:])

@@ -23,6 +23,7 @@ GROUPS = TILES // GROUP
 WORDS = HID // 2
 PAIR = 2
 CLAMP = 2.0
+RUN = 8
 PICK = P // TILES
 LAST_S = 2 * (GROUPS - 1)
 FLOPS = 2 * 2 * ROWS * HID * (HID + HALF)
@@ -74,10 +75,11 @@ def tile_affinecouplinglayer_pa_kernel(
         z_rows = [keep.tile([P, GROUP * 2 * HALF], BF16, name="z_rows%d" % g) for g in range(GROUPS)]
 
         def load_w1(n):
-            for q in range(2):
+            for first, count in ((0, 1), (1, 1), (2, 2)) if n == 0 else ((0, 2), (2, 2)):
+                at = first % PAIR
                 nc.sync.dma_start(
-                    out=w1_rows[n][q][:].rearrange("m (t k) -> m t k", t=PAIR),
-                    in_=w1_view[n][:, PAIR * q : PAIR * (q + 1), :],
+                    out=w1_rows[n][first // PAIR][:].rearrange("m (t k) -> m t k", t=PAIR)[:, at : at + count, :],
+                    in_=w1_view[n][:, first : first + count, :],
                 )
 
         def load_h(g, n):
@@ -241,8 +243,8 @@ def tile_affinecouplinglayer_pa_kernel(
                 if t == 0:
                     live[("g", v)] = work.tile([P, PACK * width(v)], BF16, name="g", tag="g")
                 nc.scalar.activation(
-                    out=live[("g", v)][:, t * width(v) : (t + 1) * width(v)],
-                    in_=live[("acc", v, t)][:],
+                    out=live[("g", v)][:].rearrange("p (c t r) -> p c t r", t=PACK, r=RUN)[:, :, t, :],
+                    in_=live[("acc", v, t)][:].rearrange("p (c r) -> p c r", r=RUN),
                     func=FN.Relu,
                     bias=b1[PARTS[v][0]][:, t : t + 1],
                 )
@@ -251,8 +253,8 @@ def tile_affinecouplinglayer_pa_kernel(
             if is_unit(v):
                 grouped = work.tile([P, width(v) * PACK], BF16, name="g_grouped", tag="g_grouped", align_bytes=64)
                 nc.vector.tensor_copy(
-                    out=grouped[:].rearrange("p (c r t) -> p c t r", r=4, t=PACK),
-                    in_=live[("g", v)][:].rearrange("p (t c r) -> p c t r", t=PACK, r=4),
+                    out=grouped[:].rearrange("p (c r t) -> p c t r", r=RUN, t=PACK),
+                    in_=live[("g", v)][:].rearrange("p (c t r) -> p c t r", t=PACK, r=RUN),
                 )
                 live[("g_grouped", v)] = grouped
 

from contextlib import ExitStack

import concourse.mybir as mybir
from concourse.masks import make_identity

BF16 = mybir.dt.bfloat16
F32 = mybir.dt.float32
U32 = mybir.dt.uint32
U8 = mybir.dt.uint8
FP8X4 = mybir.dt.float8_e4m3fn_x4
ALU = mybir.AluOpType
FN = mybir.ActivationFunctionType

P = 128
PACK = 4
ROWS = 2048
HID = 512
HALF = 128
TILES = ROWS // P
GROUP = 4
COLS = GROUP * P
GROUPS = TILES // GROUP
WORDS = HID // 2
PAIR = 2
CLAMP = 2.0
RUN = 8
PICK = P // TILES
LAST_S = 2 * (GROUPS - 1)
FLOPS = 2 * 2 * ROWS * HID * (HID + HALF)
PARTS = [(n, g * GROUP, GROUP) for g in range(GROUPS) for n in range(2)]
PARTS[-1:] = [(1, 12, 4)]
UNITS = len(PARTS)


def tile_affinecouplinglayer_pa_kernel(
    tc, z, h_s, h_t, s_Whid1, s_bhid1, s_Wout, s_bout, t_Whid1, t_bhid1, t_Wout, t_bout, out_0, out_1
):
    nc = tc.nc
    h_in = (h_s, h_t)
    w1_in = (s_Whid1, t_Whid1)
    b1_in = (s_bhid1, t_bhid1)
    wo_in = (s_Wout, t_Wout)

    with ExitStack() as ctx:
        keep = ctx.enter_context(tc.tile_pool(name="keep", bufs=1))
        work = ctx.enter_context(tc.tile_pool(name="work", bufs=2))
        small = ctx.enter_context(tc.psum_pool(name="small", bufs=3))
        acc1 = ctx.enter_context(tc.psum_pool(name="acc1", bufs=3))
        acc2 = ctx.enter_context(tc.psum_pool(name="acc2", bufs=1))
        ctx.enter_context(tc.manual_schedule())

        ident = keep.tile([P, P], F32, name="ident")
        make_identity(nc, ident[:])
        warm_in = keep.tile([P, 1], F32, name="warm_in")
        warm_out = keep.tile([P, 1], F32, name="warm_out")
        nc.vector.memset(warm_in[:], 0.0)
        ones_bf = keep.tile([P, P], BF16, name="ones_bf")
        nc.vector.memset(ones_bf[:], 1.0)
        picks = keep.tile([P, 2 * P - PICK], F32, name="picks")
        nc.vector.memset(picks[:], 0.0)
        nc.vector.memset(picks[:, P - PICK : P], 1.0)
        bt_rows = keep.tile([P, HALF], BF16, name="bt_rows")
        nc.vector.memset(bt_rows[:], 0.0)

        h_view = [h_in[n].rearrange("(p i) k -> p i k", i=TILES) for n in range(2)]
        w1_view = [w1_in[n].rearrange("(m t) k -> m t k", t=PACK) for n in range(2)]
        z_view = z.rearrange("(p i) d -> p i d", i=TILES)
        z_out_view = out_0.rearrange("(p i) d -> p i d", i=TILES)

        w1_rows = [[keep.tile([P, PAIR * HID], BF16, name="w1_rows%d_%d" % (n, q)) for q in range(2)] for n in range(2)]
        h_rows = [[keep.tile([P, PAIR * HID], BF16, name="h_rows%d_%d" % (n, q)) for q in range(TILES // PAIR)] for n in range(2)]
        b1 = [keep.tile([P, PACK], BF16, name="b1_%d" % n) for n in range(2)]
        wo_rows = [keep.tile([P, HID], BF16, name="wo_rows%d" % n) for n in range(2)]
        bs = keep.tile([P, 1], BF16, name="bs")
        z_rows = [keep.tile([P, GROUP * 2 * HALF], BF16, name="z_rows%d" % g) for g in range(GROUPS)]

        def load_w1(n):
            for first, count in ((0, 1), (1, 1), (2, 2)) if n == 0 else ((0, 2), (2, 2)):
                at = first % PAIR
                nc.sync.dma_start(
                    out=w1_rows[n][first // PAIR][:].rearrange("m (t k) -> m t k", t=PAIR)[:, at : at + count, :],
                    in_=w1_view[n][:, first : first + count, :],
                )

        def load_h(g, n):
            for q in range(2 * g, 2 * g + 2):
                nc.sync.dma_start(
                    out=h_rows[n][q][:].rearrange("p (j k) -> p j k", j=PAIR),
                    in_=h_view[n][:, PAIR * q : PAIR * (q + 1), :],
                )

        def load_z(g):
            nc.sync.dma_start(
                out=z_rows[g][:].rearrange("p (j d) -> p j d", j=GROUP),
                in_=z_view[:, g * GROUP : (g + 1) * GROUP, :],
            )

        nc.scalar.dma_start(out=bt_rows[0:1, :], in_=t_bout.rearrange("(o c) -> o c", o=1))
        nc.scalar.dma_start(out=bs[:], in_=s_bout.rearrange("(o c) -> o c", c=1))
        for n in range(2):
            nc.scalar.dma_start(out=b1[n][:], in_=b1_in[n].rearrange("(m t) -> m t", t=PACK))
        nc.scalar.activation(out=warm_out[:], in_=warm_in[:], func=FN.Exp)
        load_w1(0)
        load_h(0, 0)
        for n in range(2):
            nc.sync.dma_start(out=wo_rows[n][:], in_=wo_in[n])
        load_w1(1)
        load_h(0, 1)
        for g in range(1, GROUPS):
            load_h(g, 0)
            load_h(g, 1)
            load_z(g - 1)
        load_z(GROUPS - 1)

        w1_grouped = [keep.tile([P, PACK * HID], BF16, name="w1_grouped%d" % n, align_bytes=64) for n in range(2)]
        w1_codes = [keep.tile([P, HID], U32, name="w1_codes%d" % n, align_bytes=64) for n in range(2)]
        w1_scales = [keep.tile([P, HID], U8, name="w1_scales%d" % n, align_bytes=64) for n in range(2)]
        wo_grouped = keep.tile([P, 2 * HALF * PACK], BF16, name="wo_grouped", align_bytes=64)
        wo_codes = keep.tile([P, 2 * HALF], U32, name="wo_codes", align_bytes=64)
        wo_scales = keep.tile([P, 2 * HALF], U8, name="wo_scales", align_bytes=64)
        bias_row = keep.tile([P, HALF + 1], F32, name="bias_row")
        clamp_lo = keep.tile([P, 1], F32, name="clamp_lo")
        clamp_hi = keep.tile([P, 1], F32, name="clamp_hi")
        log_det = keep.tile([P, TILES], F32, name="log_det")
        live = {}

        def is_unit(v):
            return 0 <= v < UNITS

        def is_s(v):
            return is_unit(v) and PARTS[v][0] == 0

        def is_t(v):
            return is_unit(v) and PARTS[v][0] == 1

        def width(v):
            return PARTS[v][2] * P

        def group(v):
            return PARTS[v][1] // GROUP

        def transpose_words(rows):
            words = rows[:].bitcast(F32)
            bank = small.tile([P, COLS], F32, name="bank", tag="small")
            for j in range(2):
                for u in range(2):
                    nc.tensor.transpose(
                        bank[:, (2 * u + j) * P : (2 * u + j + 1) * P],
                        words[:, j * WORDS + u * P : j * WORDS + (u + 1) * P],
                        ident[:],
                    )
            return bank

        def interleave(copy, bank, grouped, first):
            copy(
                out=grouped[:].bitcast(F32)[:, first * 2 * P : (first + 2) * 2 * P].rearrange("p (c u) -> p c u", u=2),
                in_=bank[:].rearrange("p (u c) -> p c u", u=2),
            )

        def quantise(grouped, codes, scales):
            nc.vector.quantize_mx(out=codes[:].bitcast(FP8X4), scales=scales[:], in_=grouped[:])

        def by_tile(ap):
            return ap.rearrange("p (j c) -> p j c", c=P)

        def z_part(z_tile, part):
            return z_tile[:].rearrange("p (j d) -> p j d", d=2 * HALF)[:, :, part * HALF : (part + 1) * HALF]

        def store(first, count, part, half):
            nc.sync.dma_start(
                out=z_out_view[:, first : first + count, part * HALF : (part + 1) * HALF], in_=by_tile(half)
            )

        def w1_transposes(n):
            live[("w1_bank", n)] = [transpose_words(w1_rows[n][q]) for q in range(2)]

        def w1_copies(n, copies):
            for q in range(2):
                interleave(copies[q], live[("w1_bank", n)][q], w1_grouped[n], PAIR * q)

        def w1_quantise(n):
            quantise(w1_grouped[n], w1_codes[n], w1_scales[n])

        def wout_transposes():
            bank = small.tile([P, COLS], F32, name="bank", tag="small")
            for n in range(2):
                words = wo_rows[n][:].bitcast(F32).rearrange("c (p u) -> c p u", u=2)
                for u in range(2):
                    nc.tensor.transpose(bank[:, (2 * u + n) * P : (2 * u + n + 1) * P], words[:, :, u], ident[:])
            live["wo_bank"] = bank

        def wout_copy(copy):
            interleave(copy, live["wo_bank"], wo_grouped, 0)

        def wout_quantise():
            quantise(wo_grouped, wo_codes, wo_scales)

        def bias_matmuls():
            bank = small.tile([P, COLS], F32, name="bank", tag="small")
            nc.tensor.matmul(out=bank[:, 0:HALF], lhsT=ones_bf[:], rhs=bt_rows[:], start=True, stop=True)
            nc.tensor.matmul(out=bank[:, HALF : HALF + 1], lhsT=ones_bf[:], rhs=bs[:], start=True, stop=True)
            nc.vector.tensor_copy(out=bias_row[:], in_=bank[:, 0 : HALF + 1])
            for bound, value in ((clamp_lo, -CLAMP), (clamp_hi, CLAMP)):
                nc.vector.tensor_scalar(out=bound[:], in0=bs[:], scalar1=-1.0, scalar2=value, op0=ALU.mult, op1=ALU.add)

        def h_transposes(v):
            if is_unit(v):
                n, first, count = PARTS[v]
                live[("h_grouped", v)] = work.tile([P, width(v) * PACK], BF16, name="h_grouped", tag="h_grouped", align_bytes=64)
                live[("h_bank", v)] = [transpose_words(h_rows[n][first // PAIR + q]) for q in range(count // PAIR)]

        def h_copies(v):
            if is_unit(v):
                for pair, bank in enumerate(live[("h_bank", v)]):
                    copy = nc.vector.tensor_copy if v in (1, 3) else nc.scalar.copy
                    interleave(copy, bank, live[("h_grouped", v)], PAIR * pair)

        def h_quantise(v):
            if is_unit(v):
                codes = work.tile([P, width(v)], U32, name="h_codes", tag="h_codes", bufs=3, align_bytes=64)
                scales = work.tile([P, width(v)], U8, name="h_scales", tag="h_scales", bufs=3, align_bytes=64)
                quantise(live[("h_grouped", v)], codes, scales)
                live[("h_codes", v)] = (codes, scales)

        def layer1(v, t):
            if is_unit(v):
                n = PARTS[v][0]
                codes, scales = live[("h_codes", v)]
                acc = acc1.tile([P, width(v)], F32, name="acc", tag="acc1")
                nc.tensor.matmul_mx(
                    out=acc[:],
                    lhsT=w1_codes[n][:, t * P : (t + 1) * P].bitcast(FP8X4),
                    lhsT_scale=w1_scales[n][:, t * P : (t + 1) * P],
                    rhs=codes[:].bitcast(FP8X4),
                    rhs_scale=scales[:],
                    start=True,
                    stop=True,
                )
                live[("acc", v, t)] = acc

        def relu_out(v, t):
            if is_unit(v):
                if t == 0:
                    live[("g", v)] = work.tile([P, PACK * width(v)], BF16, name="g", tag="g")
                nc.scalar.activation(
                    out=live[("g", v)][:].rearrange("p (c t r) -> p c t r", t=PACK, r=RUN)[:, :, t, :],
                    in_=live[("acc", v, t)][:].rearrange("p (c r) -> p c r", r=RUN),
                    func=FN.Relu,
                    bias=b1[PARTS[v][0]][:, t : t + 1],
                )

        def regroup(v):
            if is_unit(v):
                grouped = work.tile([P, width(v) * PACK], BF16, name="g_grouped", tag="g_grouped", align_bytes=64)
                nc.vector.tensor_copy(
                    out=grouped[:].rearrange("p (c r t) -> p c t r", r=RUN, t=PACK),
                    in_=live[("g", v)][:].rearrange("p (c t r) -> p c t r", t=PACK, r=RUN),
                )
                live[("g_grouped", v)] = grouped

        def g_quantise(v):
            if is_unit(v):
                codes = work.tile([P, width(v)], U32, name="g_codes", tag="g_codes", align_bytes=64)
                scales = work.tile([P, width(v)], U8, name="g_scales", tag="g_scales", align_bytes=64)
                quantise(live[("g_grouped", v)], codes, scales)
                live[("g_codes", v)] = (codes, scales)

        def layer2(v):
            if is_s(v):
                codes, scales = live[("g_codes", v)]
                product = acc2.tile([P, COLS], F32, name="o_s", tag="o_s")
                nc.tensor.matmul_mx(
                    out=product[:],
                    lhsT=wo_codes[:, 0:HALF].bitcast(FP8X4),
                    lhsT_scale=wo_scales[:, 0:HALF],
                    rhs=codes[:].bitcast(FP8X4),
                    rhs_scale=scales[:],
                    start=True,
                    stop=True,
                )
                live[("o", v)] = product
            if is_t(v):
                codes, scales = live[("g_codes", v)]
                if v == UNITS - 1 and width(v) < COLS:
                    product = acc1.tile([P, width(v)], F32, name="acc", tag="acc1")
                else:
                    product = acc2.tile([P, width(v)], F32, name="o_t", tag="o_t")
                for j in range(PARTS[v][2]):
                    nc.tensor.matmul_mx(
                        out=product[:, j * P : (j + 1) * P],
                        lhsT=codes[:, j * P : (j + 1) * P].bitcast(FP8X4),
                        lhsT_scale=scales[:, j * P : (j + 1) * P],
                        rhs=wo_codes[:, HALF : 2 * HALF].bitcast(FP8X4),
                        rhs_scale=wo_scales[:, HALF : 2 * HALF],
                        start=True,
                        stop=True,
                    )
                live[("o", v)] = product

        def clamp(v):
            if is_s(v):
                unbiased = work.tile([P, COLS], F32, name="unbiased", tag="unbiased")
                nc.vector.tensor_scalar(
                    out=unbiased[:],
                    in0=live[("o", v)][:],
                    scalar1=clamp_lo[:, 0:1],
                    scalar2=clamp_hi[:, 0:1],
                    op0=ALU.max,
                    op1=ALU.min,
                )
                live[("unbiased", v)] = unbiased

        def exp(v):
            if is_s(v):
                scale = work.tile([P, COLS], F32, name="scale", tag="scale")
                nc.scalar.activation(out=scale[:], in_=live[("unbiased", v)][:], func=FN.Exp, bias=bs[:, 0:1])
                live[("scale", v)] = scale

        def row_sums(v):
            if is_s(v):
                for j in range(GROUP):
                    at = P - PICK - (PARTS[v][1] + j) * PICK
                    nc.tensor.matmul(
                        out=live[("o", v)][:, 0:P],
                        lhsT=picks[:, at : at + P],
                        rhs=live[("unbiased", v)][:, j * P : (j + 1) * P],
                        start=j == 0,
                        stop=j == GROUP - 1,
                    )

        def row_sums_exit(v):
            if is_s(v):
                sums = work.tile([P, P], F32, name="sums", tag="sums")
                if "sums" in live:
                    nc.vector.tensor_tensor(out=sums[:], in0=live[("o", v)][:, 0:P], in1=live["sums"][:], op=ALU.add)
                else:
                    nc.vector.tensor_copy(out=sums[:], in_=live[("o", v)][:, 0:P])
                live["sums"] = sums

        def row_sums_turn(v):
            if v == LAST_S:
                bank = small.tile([P, COLS], F32, name="bank", tag="small")
                nc.tensor.transpose(bank[:, 0:P], live["sums"][:], ident[:])
                live["turned"] = bank

        def row_sums_store(v):
            if v == LAST_S:
                nc.vector.tensor_scalar(
                    out=log_det[:],
                    in0=live["turned"][:, 0:P].rearrange("p (i c) -> p i c", c=PICK)[:, :, 0],
                    scalar1=bias_row[:, HALF : HALF + 1],
                    scalar2=0.0,
                    op0=ALU.add,
                    op1=ALU.add,
                )
                nc.sync.dma_start(out=out_1.rearrange("(p i) -> p i", i=TILES), in_=log_det[:])

        def exp_back(v):
            if is_s(v):
                bank = small.tile([P, COLS], F32, name="bank", tag="small")
                for j in range(GROUP):
                    nc.tensor.transpose(
                        bank[:, j * P : (j + 1) * P], live[("scale", v)][:, j * P : (j + 1) * P], ident[:]
                    )
                live[("scale_bank", v)] = bank

        def times_z2(v):
            if is_s(v):
                scaled = work.tile([P, COLS], F32, name="scaled", tag="scaled")
                nc.vector.tensor_tensor(
                    out=by_tile(scaled[:]), in0=by_tile(live[("scale_bank", v)][:]), in1=z_part(z_rows[group(v)], 1), op=ALU.mult
                )
                live[("scaled", v)] = scaled

        def add_bias(v):
            if is_s(v):
                biased = work.tile([P, COLS], F32, name="biased", tag="biased")
                nc.vector.tensor_tensor(
                    out=by_tile(biased[:]),
                    in0=by_tile(live[("scaled", v)][:]),
                    in1=bias_row[:, 0:HALF].unsqueeze(1).to_broadcast([P, GROUP, HALF]),
                    op=ALU.add,
                )
                live[("biased", group(v))] = biased

        def add_and_store(v):
            if is_t(v):
                n, first, count = PARTS[v]
                z2_out = keep.tile([P, width(v)], F32, name="z2_out%d" % v)
                at = (first % GROUP) * P
                nc.vector.tensor_tensor(
                    out=z2_out[:], in0=live[("o", v)][:], in1=live[("biased", group(v))][:, at : at + width(v)], op=ALU.add
                )
                store(first, count, 1, z2_out[:])

        def cast_z1(g):
            if 0 <= g < GROUPS:
                z1_out = keep.tile([P, COLS], F32, name="z1_out%d" % g)
                nc.scalar.copy(out=by_tile(z1_out[:]), in_=z_part(z_rows[g], 0))
                store(g * GROUP, GROUP, 0, z1_out[:])

        A, V = nc.scalar.copy, nc.vector.tensor_copy
        w1_transposes(0)
        w1_copies(0, (A, V))
        h_transposes(0)
        w1_quantise(0)
        h_copies(0)
        wout_transposes()
        h_quantise(0)
        w1_transposes(1)
        wout_copy(V)
        wout_quantise()
        layer1(0, 0)
        layer1(0, 1)
        w1_copies(1, (A, A))
        h_transposes(1)
        w1_quantise(1)
        h_copies(1)
        bias_matmuls()
        for i in range(UNITS + 4):
            relu_out(i, 0)
            times_z2(i - 3)
            layer1(i, 2)
            relu_out(i, 1)
            layer1(i, 3)
            add_and_store(i - 3)
            h_quantise(i + 1)
            g_quantise(i - 1)
            h_transposes(i + 2)
            row_sums(i - 2)
            relu_out(i, 2)
            relu_out(i, 3)
            exp(i - 2)
            h_copies(i + 2)
            layer1(i + 1, 0)
            layer1(i + 1, 1)
            exp_back(i - 2)
            row_sums_turn(i - 3)
            layer2(i - 1)
            row_sums_store(i - 3)
            add_bias(i - 3)
            clamp(i - 1)
            row_sums_exit(i - 2)
            regroup(i)
            cast_z1(i - (UNITS - 2))
